import numpy as np
import ml_dtypes


def mxq(x, axis, fmt="e4m3"):
    dtype, down = {"e4m3": (ml_dtypes.float8_e4m3fn, 7), "e5m2": (ml_dtypes.float8_e5m2, 14)}[fmt]
    v = np.moveaxis(np.asarray(x, np.float32).astype(ml_dtypes.bfloat16).astype(np.float64), axis, -1)
    blocks = v.reshape(v.shape[:-1] + (-1, 32))
    amax = np.abs(blocks).max(-1, keepdims=True)
    byte = np.maximum(np.where(amax > 0, np.frexp(amax)[1] - 1 + 127, 0) - down, 1)
    scale = np.exp2(byte - 127.0)
    codes = (blocks / scale).astype(np.float32).astype(dtype).astype(np.float64)
    return np.moveaxis((codes * scale).reshape(v.shape), -1, axis)


WIDE = False


def mx_kscale(k):
    if not WIDE:
        return np.ones(k)
    levels = np.array([10, -10, 5, -5, 0])
    a = np.random.permutation(np.resize(levels, k // 512 * 4)).reshape(k // 512, 4)
    idx = np.arange(k)
    return np.exp2(a[idx // 512, idx % 128 // 32])


BF16 = ml_dtypes.bfloat16


def bf(x):
    return np.asarray(x, np.float32).astype(BF16)


def f64(x):
    return np.asarray(x).astype(np.float64)


B, EMBED, DETER, STOC, HID, ACT = 512, 1536, 1024, 64, 1024, 12
DIST = 2 * STOC
CAT = DETER + EMBED


def softplus(v):
    return np.maximum(v, 0.0) + np.log(1.0 + np.exp(-np.abs(v)))


def setup_inputs():
    s = mx_kscale(CAT)
    tp, tq = mx_kscale(HID), mx_kscale(HID)
    r = np.random.standard_normal
    return {
        "h": bf(r((B, DETER)) * 0.65 * s[:DETER]),
        "embedding": bf(r((B, EMBED)) * s[DETER:]),
        "wp1": bf(r((HID, DETER)) / np.sqrt(DETER) / s[:DETER] * tp[:, None]),
        "bp1": bf(r(HID) * 0.1 * tp),
        "wp2": bf(r((DIST, HID)) / np.sqrt(HID) / tp),
        "bp2": bf(r(DIST) * 0.1),
        "wq1": bf(r((HID, CAT)) / np.sqrt(CAT) / s * tq[:, None]),
        "bq1": bf(r(HID) * 0.1 * tq),
        "wq2": bf(r((DIST, HID)) / np.sqrt(HID) / tq),
        "bq2": bf(r(DIST) * 0.1),
    }


def reference(h, embedding, wp1, bp1, wp2, bp2, wq1, bq1, wq2, bq2):
    cq = mxq(np.concatenate([f64(h), f64(embedding)], -1), 1, "e4m3")
    ap = np.maximum((cq[:, :DETER] @ mxq(f64(wp1), 1, "e4m3").T) + f64(bp1), 0.0)
    prior = (mxq(ap, 1, "e4m3") @ mxq(f64(wp2), 1, "e4m3").T) + f64(bp2)
    prior_mean, prior_std = np.split(prior, 2, axis=-1)
    prior_std = softplus(prior_std) + 0.1
    aq = np.maximum((cq @ mxq(f64(wq1), 1, "e4m3").T) + f64(bq1), 0.0)
    post = (mxq(aq, 1, "e4m3") @ mxq(f64(wq2), 1, "e4m3").T) + f64(bq2)
    post_mean, post_std = np.split(post, 2, axis=-1)
    post_std = softplus(post_std) + 0.1
    return (post_mean, post_std, prior_mean, prior_std)

@@ -1,0 +1,281 @@
+from contextlib import ExitStack
+
+import concourse.mybir as mybir
+from concourse.masks import make_identity
+
+F32 = mybir.dt.float32
+BF16 = mybir.dt.bfloat16
+U32 = mybir.dt.uint32
+U8 = mybir.dt.uint8
+FP8X4 = mybir.dt.float8_e4m3fn_x4
+ACT = mybir.ActivationFunctionType
+ALU = mybir.AluOpType
+
+P = 128
+PACK = 4
+K_PASS = P * PACK
+PASS_WORDS = K_PASS // 2
+
+BATCH, DETER, EMBED, HID, DIST = 512, 1024, 1536, 1024, 128
+STOC = DIST // 2
+ROW_TILES = BATCH // P
+H_PASSES = DETER // K_PASS
+C_PASSES = (DETER + EMBED) // K_PASS
+HID_PASSES = HID // K_PASS
+UNITS = HID // (2 * P)
+
+FLOPS = 2 * BATCH * (DETER * HID + (DETER + EMBED) * HID + 2 * HID * DIST)
+
+
+def tile_rssmcell_pb_kernel(
+    tc, h, embedding, wp1, bp1, wp2, bp2, wq1, bq1, wq2, bq2, post_mean, post_std, prior_mean, prior_std
+):
+    nc = tc.nc
+    with ExitStack() as ctx:
+        ctx.enter_context(tc.manual_schedule())
+        keep = ctx.enter_context(tc.tile_pool(name="keep", bufs=1))
+        ring = ctx.enter_context(tc.tile_pool(name="ring", bufs=2))
+        turned = ctx.enter_context(tc.psum_pool(name="turned", bufs=5))
+        sums = ctx.enter_context(tc.psum_pool(name="sums", bufs=3))
+
+        prior = dict(name="prior", slot=0, passes=H_PASSES, w1=wp1, b1=bp1, w2=wp2, b2=bp2, mean=prior_mean, std=prior_std)
+        post = dict(name="post", slot=1, passes=C_PASSES, w1=wq1, b1=bq1, w2=wq2, b2=bq2, mean=post_mean, std=post_std)
+
+        h_rows = keep.tile([P, ROW_TILES, DETER], BF16, name="h_rows")
+        e_rows = keep.tile([P, ROW_TILES, EMBED], BF16, name="e_rows")
+
+        def load_batch_rows(rows, source):
+            view = source.rearrange("(p t) k -> p t k", t=ROW_TILES)
+            for half in range(2):
+                nc.sync.dma_start(out=rows[:, 2 * half : 2 * half + 2, :], in_=view[:, 2 * half : 2 * half + 2, :])
+
+        def load_unit(head, unit):
+            features = head["passes"] * K_PASS
+            rows = keep.tile([P, 2, features], BF16, name="%s_rows%d" % (head["name"], unit))
+            view = head["w1"].rearrange("(g p c i) k -> g c p i k", g=HID_PASSES, p=P, c=2, i=2)
+            nc.sync.dma_start(out=rows[:], in_=view[unit // 2, unit % 2])
+            return rows
+
+        for head in (prior, post):
+            bias1_bf = keep.tile([P, HID_PASSES, PACK], BF16, name="%s_bias1_bf" % head["name"])
+            nc.scalar.dma_start(out=bias1_bf[:], in_=head["b1"].rearrange("(g p j) -> p g j", g=HID_PASSES, p=P, j=PACK))
+            head["bias1_bf"] = bias1_bf
+
+        load_batch_rows(h_rows, h)
+        prior["rows"] = [load_unit(prior, unit) for unit in range(UNITS)]
+        load_batch_rows(e_rows, embedding)
+        post["rows"] = [load_unit(post, unit) for unit in range(UNITS)]
+        bias2 = keep.tile([P, 2, DIST], BF16, name="bias2")
+        for head in (prior, post):
+            w2_rows = keep.tile([P, HID], BF16, name="%s_w2_rows" % head["name"])
+            nc.sync.dma_start(out=w2_rows[:], in_=head["w2"])
+            head["w2_rows"] = w2_rows
+        for head in (prior, post):
+            nc.sync.dma_start(out=bias2[:, head["slot"], :], in_=head["b2"].partition_broadcast(P))
+
+        ident = keep.tile([P, P], F32, name="ident")
+        make_identity(nc, ident[:])
+        zero = keep.tile([P, 1], F32, name="zero")
+        one = keep.tile([P, 1], F32, name="one")
+        nc.vector.memset(zero[:], 0.0)
+        nc.scalar.activation(out=one[:], in_=zero[:], func=ACT.Exp)
+
+        def turn_bank(blocks):
+            bank = turned.tile([P, 2, 2, P], F32, name="bank")
+            for i in range(2):
+                for u in range(2):
+                    nc.tensor.transpose(bank[:, i, u, :], blocks[i][u], ident[:])
+            return bank
+
+        def pass_blocks(words, g):
+            return [
+                [words[:, i, PASS_WORDS * g + P * u : PASS_WORDS * g + P * u + P] for u in range(2)]
+                for i in range(2)
+            ]
+
+        def copy_bank(engine_copy, bank, grouped_words):
+            engine_copy(out=grouped_words, in_=bank[:].rearrange("p i u r -> p i r u"))
+
+        c_codes = keep.tile([P, C_PASSES, BATCH], U32, name="c_codes", align_bytes=64)
+        c_scales = keep.tile([P, C_PASSES, BATCH], U8, name="c_scales", align_bytes=64)
+
+        def turn_batch_rows(rows, first_pass, passes):
+            words = rows[:].bitcast(F32)
+            grouped = [
+                ring.tile([P, ROW_TILES, P, PACK], BF16, name="grouped_c", bufs=3, align_bytes=64)
+                for g in range(passes)
+            ]
+            for half in range(2):
+                for g in range(passes):
+                    bank = turn_bank(pass_blocks(words[:, 2 * half : 2 * half + 2, :], g))
+                    engine_copy = nc.scalar.copy if (half * passes + g) % 3 != 2 else nc.vector.tensor_copy
+                    copy_bank(engine_copy, bank, grouped[g][:].bitcast(F32)[:, 2 * half : 2 * half + 2, :, :])
+            for g in range(passes):
+                nc.vector.quantize_mx(
+                    out=c_codes[:, first_pass + g, :].bitcast(FP8X4),
+                    scales=c_scales[:, first_pass + g, :],
+                    in_=grouped[g][:].rearrange("p t r j -> p (t r j)"),
+                )
+
+        def turn_unit(head, unit):
+            passes = head["passes"]
+            words = head["rows"][unit][:].bitcast(F32)
+            codes = keep.tile([P, passes, 2 * P], U32, name="%s_codes%d" % (head["name"], unit), align_bytes=64)
+            scales = keep.tile([P, passes, 2 * P], U8, name="%s_scales%d" % (head["name"], unit), align_bytes=64)
+            grouped = []
+            for g in range(passes):
+                bank = turn_bank(pass_blocks(words, g))
+                grouped_w = ring.tile([P, 2, P, PACK], BF16, name="grouped_w", bufs=10, align_bytes=64)
+                copy_bank(nc.scalar.copy, bank, grouped_w[:].bitcast(F32))
+                grouped.append(grouped_w)
+            for g in range(passes):
+                nc.vector.quantize_mx(
+                    out=codes[:, g, :].bitcast(FP8X4),
+                    scales=scales[:, g, :],
+                    in_=grouped[g][:].rearrange("p i r j -> p (i r j)"),
+                )
+            head["codes%d" % unit] = codes
+            head["scales%d" % unit] = scales
+
+        def turn_second_weight(head):
+            words = head["w2_rows"][:].bitcast(F32).rearrange("d (g p u) -> d g u p", g=HID_PASSES, p=P, u=2)
+            bank = turn_bank([[words[:, g, u, :] for u in range(2)] for g in range(HID_PASSES)])
+            grouped_w = ring.tile([P, 2, P, PACK], BF16, name="grouped_w", bufs=10, align_bytes=64)
+            copy_bank(nc.scalar.copy, bank, grouped_w[:].bitcast(F32))
+            codes = keep.tile([P, HID_PASSES, DIST], U32, name="%s_w2_codes" % head["name"], align_bytes=64)
+            scales = keep.tile([P, HID_PASSES, DIST], U8, name="%s_w2_scales" % head["name"], align_bytes=64)
+            nc.vector.quantize_mx(
+                out=codes[:].rearrange("p g d -> p (g d)").bitcast(FP8X4),
+                scales=scales[:].rearrange("p g d -> p (g d)"),
+                in_=grouped_w[:].rearrange("p g d j -> p (g d j)"),
+            )
+            head["w2_codes"] = codes
+            head["w2_scales"] = scales
+
+        for head in (prior, post):
+            head["bias1"] = keep.tile([P, HID_PASSES, PACK], F32, name="%s_bias1" % head["name"])
+            head["hidden"] = [
+                keep.tile([P, PACK, BATCH], BF16, name="%s_hidden%d" % (head["name"], g)) for g in range(HID_PASSES)
+            ]
+            head["a_codes"] = keep.tile([P, HID_PASSES, BATCH], U32, name="%s_a_codes" % head["name"], align_bytes=64)
+            head["a_scales"] = keep.tile([P, HID_PASSES, BATCH], U8, name="%s_a_scales" % head["name"], align_bytes=64)
+
+        def first_layer(head, unit):
+            passes = head["passes"]
+            codes, scales = head["codes%d" % unit], head["scales%d" % unit]
+            for i in range(2):
+                total = sums.tile([P, BATCH], F32, name="total")
+                for g in range(passes):
+                    nc.tensor.matmul_mx(
+                        out=total[:],
+                        lhsT=codes[:, g, P * i : P * i + P].bitcast(FP8X4),
+                        lhsT_scale=scales[:, g, P * i : P * i + P],
+                        rhs=c_codes[:, g, :].bitcast(FP8X4),
+                        rhs_scale=c_scales[:, g, :],
+                        start=(g == 0),
+                        stop=(g == passes - 1),
+                    )
+                j = 2 * (unit % 2) + i
+                bias = head["bias1"][:, unit // 2, j : j + 1]
+                rounded = head["hidden"][unit // 2][:, j, :]
+                if i == 0:
+                    nc.scalar.activation(out=rounded, in_=total[:], func=ACT.Relu, bias=bias, scale=1.0)
+                else:
+                    nc.vector.tensor_scalar(
+                        out=rounded, in0=total[:], scalar1=bias, scalar2=0.0, op0=ALU.add, op1=ALU.max
+                    )
+
+        def group_hidden(head, g):
+            grouped_a = ring.tile([P, BATCH, PACK], BF16, name="grouped_a", bufs=2, align_bytes=64)
+            nc.vector.tensor_copy(
+                out=grouped_a[:].rearrange("p (c i) j -> p c j i", i=4),
+                in_=head["hidden"][g][:].rearrange("p j (c i) -> p c j i", i=4),
+            )
+            return grouped_a
+
+        def quantise_hidden(head, g, grouped_a):
+            nc.vector.quantize_mx(
+                out=head["a_codes"][:, g, :].bitcast(FP8X4),
+                scales=head["a_scales"][:, g, :],
+                in_=grouped_a[:].rearrange("p b j -> p (b j)"),
+            )
+
+        def second_layer(head):
+            result = sums.tile([P, ROW_TILES, DIST], F32, name="total")
+            for t in range(ROW_TILES):
+                for g in range(HID_PASSES):
+                    nc.tensor.matmul_mx(
+                        out=result[:, t, :],
+                        lhsT=head["a_codes"][:, g, P * t : P * t + P].bitcast(FP8X4),
+                        lhsT_scale=head["a_scales"][:, g, P * t : P * t + P],
+                        rhs=head["w2_codes"][:, g, :].bitcast(FP8X4),
+                        rhs_scale=head["w2_scales"][:, g, :],
+                        start=(g == 0),
+                        stop=(g == HID_PASSES - 1),
+                    )
+            return result
+
+        def spread_bias2(head, columns):
+            return bias2[:, head["slot"], columns].unsqueeze(1).to_broadcast([P, ROW_TILES, STOC])
+
+        def by_partition(out):
+            return out.rearrange("(p t) d -> p t d", t=ROW_TILES)
+
+        def begin_outputs(head, result):
+            name = head["name"]
+            v = keep.tile([P, ROW_TILES, STOC], F32, name="%s_v" % name)
+            nc.vector.tensor_tensor(
+                out=v[:], in0=result[:, :, STOC:DIST], in1=spread_bias2(head, slice(STOC, DIST)), op=ALU.add
+            )
+            size = keep.tile([P, ROW_TILES, STOC], F32, name="%s_size" % name)
+            nc.scalar.activation(out=size[:], in_=v[:], func=ACT.Abs)
+            decay = keep.tile([P, ROW_TILES, STOC], F32, name="%s_decay" % name)
+            nc.scalar.activation(out=decay[:], in_=size[:], func=ACT.Exp, scale=-1.0)
+            mean = keep.tile([P, ROW_TILES, STOC], F32, name="%s_mean" % name)
+            nc.vector.tensor_tensor(
+                out=mean[:], in0=result[:, :, 0:STOC], in1=spread_bias2(head, slice(0, STOC)), op=ALU.add
+            )
+            nc.sync.dma_start(out=by_partition(head["mean"]), in_=mean[:])
+            hinge = keep.tile([P, ROW_TILES, STOC], F32, name="%s_hinge" % name)
+            nc.vector.tensor_scalar(out=hinge[:], in0=v[:], scalar1=0.0, scalar2=0.1, op0=ALU.max, op1=ALU.add)
+            head["decay"] = decay
+            head["hinge"] = hinge
+
+        def finish_outputs(head):
+            name = head["name"]
+            log_term = keep.tile([P, ROW_TILES, STOC], F32, name="%s_log" % name)
+            nc.scalar.activation(out=log_term[:], in_=head["decay"][:], func=ACT.Ln, bias=1.0)
+            std = keep.tile([P, ROW_TILES, STOC], F32, name="%s_std" % name)
+            nc.vector.tensor_tensor(out=std[:], in0=head["hinge"][:], in1=log_term[:], op=ALU.add)
+            nc.sync.dma_start(out=by_partition(head["std"]), in_=std[:])
+
+        turn_batch_rows(h_rows, 0, H_PASSES)
+        for head in (prior, post):
+            nc.vector.tensor_copy(out=head["bias1"][:], in_=head["bias1_bf"][:])
+        turn_unit(prior, 0)
+        for unit in range(UNITS):
+            if unit + 1 < UNITS:
+                turn_unit(prior, unit + 1)
+            else:
+                turn_batch_rows(e_rows, H_PASSES, C_PASSES - H_PASSES)
+            first_layer(prior, unit)
+
+        turn_unit(post, 0)
+        turn_unit(post, 1)
+        first_layer(post, 0)
+        prior_grouped = [group_hidden(prior, g) for g in range(HID_PASSES)]
+        for g in range(HID_PASSES):
+            quantise_hidden(prior, g, prior_grouped[g])
+        turn_unit(post, 2)
+        first_layer(post, 1)
+        turn_unit(post, 3)
+        turn_second_weight(prior)
+        turn_second_weight(post)
+        first_layer(post, 2)
+        quantise_hidden(post, 0, group_hidden(post, 0))
+        begin_outputs(prior, second_layer(prior))
+        first_layer(post, 3)
+        quantise_hidden(post, 1, group_hidden(post, 1))
+        begin_outputs(post, second_layer(post))
+        finish_outputs(post)
+        finish_outputs(prior)

@@ -23,6 +23,7 @@ H_PASSES = DETER // K_PASS
 C_PASSES = (DETER + EMBED) // K_PASS
 HID_PASSES = HID // K_PASS
 UNITS = HID // (2 * P)
+HALF = BATCH // 2
 
 FLOPS = 2 * BATCH * (DETER * HID + (DETER + EMBED) * HID + 2 * HID * DIST)
 
@@ -38,8 +39,8 @@ def tile_rssmcell_pb_kernel(
         turned = ctx.enter_context(tc.psum_pool(name="turned", bufs=5))
         sums = ctx.enter_context(tc.psum_pool(name="sums", bufs=3))
 
-        prior = dict(name="prior", slot=0, passes=H_PASSES, w1=wp1, b1=bp1, w2=wp2, b2=bp2, mean=prior_mean, std=prior_std)
-        post = dict(name="post", slot=1, passes=C_PASSES, w1=wq1, b1=bq1, w2=wq2, b2=bq2, mean=post_mean, std=post_std)
+        prior = dict(name="prior", slot=0, passes=H_PASSES, w1=wp1, b1=bp1, w2=wp2, b2=bp2, mean_out=prior_mean, std_out=prior_std)
+        post = dict(name="post", slot=1, passes=C_PASSES, w1=wq1, b1=bq1, w2=wq2, b2=bq2, mean_out=post_mean, std_out=post_std)
 
         h_rows = keep.tile([P, ROW_TILES, DETER], BF16, name="h_rows")
         e_rows = keep.tile([P, ROW_TILES, EMBED], BF16, name="e_rows")
@@ -64,12 +65,13 @@ def tile_rssmcell_pb_kernel(
         load_batch_rows(h_rows, h)
         prior["rows"] = [load_unit(prior, unit) for unit in range(UNITS)]
         load_batch_rows(e_rows, embedding)
-        post["rows"] = [load_unit(post, unit) for unit in range(UNITS)]
-        bias2 = keep.tile([P, 2, DIST], BF16, name="bias2")
+        post["rows"] = [load_unit(post, unit) for unit in range(2)]
         for head in (prior, post):
             w2_rows = keep.tile([P, HID], BF16, name="%s_w2_rows" % head["name"])
             nc.sync.dma_start(out=w2_rows[:], in_=head["w2"])
             head["w2_rows"] = w2_rows
+        post["rows"].extend([load_unit(post, unit) for unit in range(2, UNITS)])
+        bias2 = keep.tile([P, 2, DIST], BF16, name="bias2")
         for head in (prior, post):
             nc.sync.dma_start(out=bias2[:, head["slot"], :], in_=head["b2"].partition_broadcast(P))
 
@@ -106,16 +108,17 @@ def tile_rssmcell_pb_kernel(
                 for g in range(passes)
             ]
             for half in range(2):
+                tiles = slice(2 * half, 2 * half + 2)
                 for g in range(passes):
-                    bank = turn_bank(pass_blocks(words[:, 2 * half : 2 * half + 2, :], g))
-                    engine_copy = nc.scalar.copy if (half * passes + g) % 3 != 2 else nc.vector.tensor_copy
-                    copy_bank(engine_copy, bank, grouped[g][:].bitcast(F32)[:, 2 * half : 2 * half + 2, :, :])
-            for g in range(passes):
-                nc.vector.quantize_mx(
-                    out=c_codes[:, first_pass + g, :].bitcast(FP8X4),
-                    scales=c_scales[:, first_pass + g, :],
-                    in_=grouped[g][:].rearrange("p t r j -> p (t r j)"),
-                )
+                    bank = turn_bank(pass_blocks(words[:, tiles, :], g))
+                    engine_copy = nc.scalar.copy if (half * passes + g) % 2 == 0 else nc.vector.tensor_copy
+                    copy_bank(engine_copy, bank, grouped[g][:].bitcast(F32)[:, tiles, :, :])
+                for g in range(passes):
+                    nc.vector.quantize_mx(
+                        out=c_codes[:, first_pass + g, HALF * half : HALF * half + HALF].bitcast(FP8X4),
+                        scales=c_scales[:, first_pass + g, HALF * half : HALF * half + HALF],
+                        in_=grouped[g][:, tiles, :, :].rearrange("p t r j -> p (t r j)"),
+                    )
 
         def turn_unit(head, unit):
             passes = head["passes"]
@@ -160,24 +163,25 @@ def tile_rssmcell_pb_kernel(
             head["a_codes"] = keep.tile([P, HID_PASSES, BATCH], U32, name="%s_a_codes" % head["name"], align_bytes=64)
             head["a_scales"] = keep.tile([P, HID_PASSES, BATCH], U8, name="%s_a_scales" % head["name"], align_bytes=64)
 
-        def first_layer(head, unit):
+        def first_layer(head, unit, first, width):
             passes = head["passes"]
             codes, scales = head["codes%d" % unit], head["scales%d" % unit]
+            columns = slice(first, first + width)
             for i in range(2):
-                total = sums.tile([P, BATCH], F32, name="total")
+                total = sums.tile([P, width], F32, name="total")
                 for g in range(passes):
                     nc.tensor.matmul_mx(
                         out=total[:],
                         lhsT=codes[:, g, P * i : P * i + P].bitcast(FP8X4),
                         lhsT_scale=scales[:, g, P * i : P * i + P],
-                        rhs=c_codes[:, g, :].bitcast(FP8X4),
-                        rhs_scale=c_scales[:, g, :],
+                        rhs=c_codes[:, g, columns].bitcast(FP8X4),
+                        rhs_scale=c_scales[:, g, columns],
                         start=(g == 0),
                         stop=(g == passes - 1),
                     )
                 j = 2 * (unit % 2) + i
                 bias = head["bias1"][:, unit // 2, j : j + 1]
-                rounded = head["hidden"][unit // 2][:, j, :]
+                rounded = head["hidden"][unit // 2][:, j, columns]
                 if i == 0:
                     nc.scalar.activation(out=rounded, in_=total[:], func=ACT.Relu, bias=bias, scale=1.0)
                 else:
@@ -185,27 +189,28 @@ def tile_rssmcell_pb_kernel(
                         out=rounded, in0=total[:], scalar1=bias, scalar2=0.0, op0=ALU.add, op1=ALU.max
                     )
 
-        def group_hidden(head, g):
-            grouped_a = ring.tile([P, BATCH, PACK], BF16, name="grouped_a", bufs=2, align_bytes=64)
+        def group_hidden(head, g, first, width):
+            grouped_a = ring.tile([P, width, PACK], BF16, name="grouped_a", bufs=2, align_bytes=64)
             nc.vector.tensor_copy(
                 out=grouped_a[:].rearrange("p (c i) j -> p c j i", i=4),
-                in_=head["hidden"][g][:].rearrange("p j (c i) -> p c j i", i=4),
+                in_=head["hidden"][g][:, :, first : first + width].rearrange("p j (c i) -> p c j i", i=4),
             )
             return grouped_a
 
-        def quantise_hidden(head, g, grouped_a):
+        def quantise_hidden(head, g, first, width, grouped_a):
             nc.vector.quantize_mx(
-                out=head["a_codes"][:, g, :].bitcast(FP8X4),
-                scales=head["a_scales"][:, g, :],
+                out=head["a_codes"][:, g, first : first + width].bitcast(FP8X4),
+                scales=head["a_scales"][:, g, first : first + width],
                 in_=grouped_a[:].rearrange("p b j -> p (b j)"),
             )
 
-        def second_layer(head):
-            result = sums.tile([P, ROW_TILES, DIST], F32, name="total")
-            for t in range(ROW_TILES):
+        def second_layer(head, first_tile, tiles):
+            result = turned.tile([P, tiles, DIST], F32, name="bank")
+            for n in range(tiles):
+                t = first_tile + n
                 for g in range(HID_PASSES):
                     nc.tensor.matmul_mx(
-                        out=result[:, t, :],
+                        out=result[:, n, :],
                         lhsT=head["a_codes"][:, g, P * t : P * t + P].bitcast(FP8X4),
                         lhsT_scale=head["a_scales"][:, g, P * t : P * t + P],
                         rhs=head["w2_codes"][:, g, :].bitcast(FP8X4),
@@ -215,31 +220,33 @@ def tile_rssmcell_pb_kernel(
                     )
             return result
 
-        def spread_bias2(head, columns):
-            return bias2[:, head["slot"], columns].unsqueeze(1).to_broadcast([P, ROW_TILES, STOC])
+        def spread_bias2(head, columns, tiles):
+            return bias2[:, head["slot"], columns].unsqueeze(1).to_broadcast([P, tiles, STOC])
 
         def by_partition(out):
             return out.rearrange("(p t) d -> p t d", t=ROW_TILES)
 
-        def begin_outputs(head, result):
-            name = head["name"]
-            v = keep.tile([P, ROW_TILES, STOC], F32, name="%s_v" % name)
+        for head in (prior, post):
+            for part in ("v", "size", "decay", "mean", "hinge"):
+                head[part] = keep.tile([P, ROW_TILES, STOC], F32, name="%s_%s" % (head["name"], part))
+
+        def begin_softplus(head, first_tile, tiles, result):
+            span = slice(first_tile, first_tile + tiles)
+            v, size, decay = [head[part][:, span, :] for part in ("v", "size", "decay")]
             nc.vector.tensor_tensor(
-                out=v[:], in0=result[:, :, STOC:DIST], in1=spread_bias2(head, slice(STOC, DIST)), op=ALU.add
+                out=v, in0=result[:, :, STOC:DIST], in1=spread_bias2(head, slice(STOC, DIST), tiles), op=ALU.add
             )
-            size = keep.tile([P, ROW_TILES, STOC], F32, name="%s_size" % name)
-            nc.scalar.activation(out=size[:], in_=v[:], func=ACT.Abs)
-            decay = keep.tile([P, ROW_TILES, STOC], F32, name="%s_decay" % name)
-            nc.scalar.activation(out=decay[:], in_=size[:], func=ACT.Exp, scale=-1.0)
-            mean = keep.tile([P, ROW_TILES, STOC], F32, name="%s_mean" % name)
+            nc.scalar.activation(out=size, in_=v, func=ACT.Abs)
+            nc.scalar.activation(out=decay, in_=size, func=ACT.Exp, scale=-1.0)
+
+        def mean_and_hinge(head, first_tile, tiles, result):
+            span = slice(first_tile, first_tile + tiles)
+            v, mean, hinge = [head[part][:, span, :] for part in ("v", "mean", "hinge")]
             nc.vector.tensor_tensor(
-                out=mean[:], in0=result[:, :, 0:STOC], in1=spread_bias2(head, slice(0, STOC)), op=ALU.add
+                out=mean, in0=result[:, :, 0:STOC], in1=spread_bias2(head, slice(0, STOC), tiles), op=ALU.add
             )
-            nc.sync.dma_start(out=by_partition(head["mean"]), in_=mean[:])
-            hinge = keep.tile([P, ROW_TILES, STOC], F32, name="%s_hinge" % name)
-            nc.vector.tensor_scalar(out=hinge[:], in0=v[:], scalar1=0.0, scalar2=0.1, op0=ALU.max, op1=ALU.add)
-            head["decay"] = decay
-            head["hinge"] = hinge
+            nc.sync.dma_start(out=by_partition(head["mean_out"])[:, span, :], in_=mean)
+            nc.vector.tensor_scalar(out=hinge, in0=v, scalar1=0.0, scalar2=0.1, op0=ALU.max, op1=ALU.add)
 
         def finish_outputs(head):
             name = head["name"]
@@ -247,7 +254,7 @@ def tile_rssmcell_pb_kernel(
             nc.scalar.activation(out=log_term[:], in_=head["decay"][:], func=ACT.Ln, bias=1.0)
             std = keep.tile([P, ROW_TILES, STOC], F32, name="%s_std" % name)
             nc.vector.tensor_tensor(out=std[:], in0=head["hinge"][:], in1=log_term[:], op=ALU.add)
-            nc.sync.dma_start(out=by_partition(head["std"]), in_=std[:])
+            nc.sync.dma_start(out=by_partition(head["std_out"]), in_=std[:])
 
         turn_batch_rows(h_rows, 0, H_PASSES)
         for head in (prior, post):
@@ -258,24 +265,38 @@ def tile_rssmcell_pb_kernel(
                 turn_unit(prior, unit + 1)
             else:
                 turn_batch_rows(e_rows, H_PASSES, C_PASSES - H_PASSES)
-            first_layer(prior, unit)
+            first_layer(prior, unit, 0, BATCH)
 
         turn_unit(post, 0)
+        grouped_a = group_hidden(prior, 0, 0, BATCH)
         turn_unit(post, 1)
-        first_layer(post, 0)
-        prior_grouped = [group_hidden(prior, g) for g in range(HID_PASSES)]
-        for g in range(HID_PASSES):
-            quantise_hidden(prior, g, prior_grouped[g])
-        turn_unit(post, 2)
-        first_layer(post, 1)
-        turn_unit(post, 3)
+        quantise_hidden(prior, 0, 0, BATCH, grouped_a)
+        first_layer(post, 0, 0, BATCH)
+
+        grouped_a = group_hidden(prior, 1, 0, BATCH)
         turn_second_weight(prior)
         turn_second_weight(post)
-        first_layer(post, 2)
-        quantise_hidden(post, 0, group_hidden(post, 0))
-        begin_outputs(prior, second_layer(prior))
-        first_layer(post, 3)
-        quantise_hidden(post, 1, group_hidden(post, 1))
-        begin_outputs(post, second_layer(post))
+        turn_unit(post, 2)
+        quantise_hidden(prior, 1, 0, BATCH, grouped_a)
+        first_layer(post, 1, 0, BATCH)
+
+        grouped_a = group_hidden(post, 0, 0, BATCH)
+        turn_unit(post, 3)
+        quantise_hidden(post, 0, 0, BATCH, grouped_a)
+        prior_result = second_layer(prior, 0, ROW_TILES)
+        first_layer(post, 2, 0, BATCH)
+
+        first_layer(post, 3, 0, HALF)
+        quantise_hidden(post, 1, 0, HALF, group_hidden(post, 1, 0, HALF))
+        first_layer(post, 3, HALF, HALF)
+        first_result = second_layer(post, 0, 2)
+        quantise_hidden(post, 1, HALF, HALF, group_hidden(post, 1, HALF, HALF))
+        second_result = second_layer(post, 2, 2)
+        begin_softplus(prior, 0, ROW_TILES, prior_result)
+        begin_softplus(post, 0, 2, first_result)
+        begin_softplus(post, 2, 2, second_result)
+        mean_and_hinge(prior, 0, ROW_TILES, prior_result)
+        mean_and_hinge(post, 0, 2, first_result)
+        mean_and_hinge(post, 2, 2, second_result)
         finish_outputs(post)
         finish_outputs(prior)

@@ -101,44 +101,40 @@ def tile_rssmcell_pb_kernel(
         c_codes = keep.tile([P, C_PASSES, BATCH], U32, name="c_codes", align_bytes=64)
         c_scales = keep.tile([P, C_PASSES, BATCH], U8, name="c_scales", align_bytes=64)
 
-        def turn_batch_rows(rows, first_pass, passes):
+        def turn_batch_rows(rows, first_pass, passes, halves):
             words = rows[:].bitcast(F32)
-            grouped = [
-                ring.tile([P, ROW_TILES, P, PACK], BF16, name="grouped_c", bufs=3, align_bytes=64)
-                for g in range(passes)
-            ]
-            for half in range(2):
+            for half in halves:
                 tiles = slice(2 * half, 2 * half + 2)
+                grouped = []
                 for g in range(passes):
                     bank = turn_bank(pass_blocks(words[:, tiles, :], g))
+                    grouped_c = ring.tile([P, 2, P, PACK], BF16, name="grouped_w", bufs=10, align_bytes=64)
+                    grouped.append(grouped_c)
                     engine_copy = nc.scalar.copy if (half * passes + g) % 2 == 0 else nc.vector.tensor_copy
-                    copy_bank(engine_copy, bank, grouped[g][:].bitcast(F32)[:, tiles, :, :])
+                    copy_bank(engine_copy, bank, grouped_c[:].bitcast(F32))
                 for g in range(passes):
                     nc.vector.quantize_mx(
                         out=c_codes[:, first_pass + g, HALF * half : HALF * half + HALF].bitcast(FP8X4),
                         scales=c_scales[:, first_pass + g, HALF * half : HALF * half + HALF],
-                        in_=grouped[g][:, tiles, :, :].rearrange("p t r j -> p (t r j)"),
+                        in_=grouped[g][:].rearrange("p t r j -> p (t r j)"),
                     )
 
-        def turn_unit(head, unit):
+        def turn_weight(head, unit, pieces, engine_copy):
             passes = head["passes"]
             words = head["rows"][unit][:].bitcast(F32)
-            codes = keep.tile([P, passes, 2 * P], U32, name="%s_codes%d" % (head["name"], unit), align_bytes=64)
-            scales = keep.tile([P, passes, 2 * P], U8, name="%s_scales%d" % (head["name"], unit), align_bytes=64)
-            grouped = []
-            for g in range(passes):
+            if unit not in head["codes"]:
+                head["codes"][unit] = keep.tile([P, passes, 2 * P], U32, name="%s_codes%d" % (head["name"], unit), align_bytes=64)
+                head["scales"][unit] = keep.tile([P, passes, 2 * P], U8, name="%s_scales%d" % (head["name"], unit), align_bytes=64)
+            codes, scales = head["codes"][unit], head["scales"][unit]
+            for g in pieces:
                 bank = turn_bank(pass_blocks(words, g))
                 grouped_w = ring.tile([P, 2, P, PACK], BF16, name="grouped_w", bufs=10, align_bytes=64)
-                copy_bank(nc.scalar.copy, bank, grouped_w[:].bitcast(F32))
-                grouped.append(grouped_w)
-            for g in range(passes):
+                copy_bank(engine_copy, bank, grouped_w[:].bitcast(F32))
                 nc.vector.quantize_mx(
                     out=codes[:, g, :].bitcast(FP8X4),
                     scales=scales[:, g, :],
-                    in_=grouped[g][:].rearrange("p i r j -> p (i r j)"),
+                    in_=grouped_w[:].rearrange("p i r j -> p (i r j)"),
                 )
-            head["codes%d" % unit] = codes
-            head["scales%d" % unit] = scales
 
         def turn_second_weight(head):
             words = head["w2_rows"][:].bitcast(F32).rearrange("d (g p u) -> d g u p", g=HID_PASSES, p=P, u=2)
@@ -156,6 +152,7 @@ def tile_rssmcell_pb_kernel(
             head["w2_scales"] = scales
 
         for head in (prior, post):
+            head["codes"], head["scales"] = {}, {}
             head["bias1"] = keep.tile([P, HID_PASSES, PACK], F32, name="%s_bias1" % head["name"])
             head["hidden"] = [
                 keep.tile([P, PACK, BATCH], BF16, name="%s_hidden%d" % (head["name"], g)) for g in range(HID_PASSES)
@@ -163,11 +160,11 @@ def tile_rssmcell_pb_kernel(
             head["a_codes"] = keep.tile([P, HID_PASSES, BATCH], U32, name="%s_a_codes" % head["name"], align_bytes=64)
             head["a_scales"] = keep.tile([P, HID_PASSES, BATCH], U8, name="%s_a_scales" % head["name"], align_bytes=64)
 
-        def first_layer(head, unit, first, width):
+        def first_layer(head, unit, tiles, first, width, alone=False):
             passes = head["passes"]
-            codes, scales = head["codes%d" % unit], head["scales%d" % unit]
+            codes, scales = head["codes"][unit], head["scales"][unit]
             columns = slice(first, first + width)
-            for i in range(2):
+            for i in tiles:
                 total = sums.tile([P, width], F32, name="total")
                 for g in range(passes):
                     nc.tensor.matmul_mx(
@@ -182,7 +179,7 @@ def tile_rssmcell_pb_kernel(
                 j = 2 * (unit % 2) + i
                 bias = head["bias1"][:, unit // 2, j : j + 1]
                 rounded = head["hidden"][unit // 2][:, j, columns]
-                if i == 0:
+                if i == 0 or alone:
                     nc.scalar.activation(out=rounded, in_=total[:], func=ACT.Relu, bias=bias, scale=1.0)
                 else:
                     nc.vector.tensor_scalar(
@@ -256,39 +253,49 @@ def tile_rssmcell_pb_kernel(
             nc.vector.tensor_tensor(out=std[:], in0=head["hinge"][:], in1=log_term[:], op=ALU.add)
             nc.sync.dma_start(out=by_partition(head["std_out"]), in_=std[:])
 
-        turn_batch_rows(h_rows, 0, H_PASSES)
+        both = (0, 1)
+        turn_batch_rows(h_rows, 0, H_PASSES, both)
         for head in (prior, post):
             nc.vector.tensor_copy(out=head["bias1"][:], in_=head["bias1_bf"][:])
-        turn_unit(prior, 0)
-        for unit in range(UNITS):
-            if unit + 1 < UNITS:
-                turn_unit(prior, unit + 1)
-            else:
-                turn_batch_rows(e_rows, H_PASSES, C_PASSES - H_PASSES)
-            first_layer(prior, unit, 0, BATCH)
-
-        turn_unit(post, 0)
-        grouped_a = group_hidden(prior, 0, 0, BATCH)
-        turn_unit(post, 1)
-        quantise_hidden(prior, 0, 0, BATCH, grouped_a)
-        first_layer(post, 0, 0, BATCH)
-
-        grouped_a = group_hidden(prior, 1, 0, BATCH)
+        S = nc.scalar.copy
+        turn_weight(prior, 0, range(2), S)
+        turn_weight(prior, 1, range(2), S)
+        first_layer(prior, 0, both, 0, BATCH)
+        turn_weight(prior, 2, range(2), S)
+        first_layer(prior, 1, both, 0, BATCH)
+        turn_weight(prior, 3, range(2), S)
+        first_layer(prior, 2, (0,), 0, BATCH)
+        turn_batch_rows(e_rows, H_PASSES, C_PASSES - H_PASSES, (0,))
+        first_layer(prior, 2, (1,), 0, BATCH)
+        turn_batch_rows(e_rows, H_PASSES, C_PASSES - H_PASSES, (1,))
+        first_layer(prior, 3, (0,), 0, BATCH)
+        turn_weight(post, 0, range(3), S)
+        first_layer(prior, 3, (1,), 0, BATCH)
+        turn_weight(post, 0, (3, 4), S)
+        turn_weight(post, 1, range(3), S)
+        first_layer(post, 0, (0,), 0, BATCH)
+        turn_weight(post, 1, (3, 4), S)
+        grouped_p0 = group_hidden(prior, 0, 0, BATCH)
+        first_layer(post, 0, (1,), 0, BATCH)
+        turn_weight(post, 2, range(3), S)
+        quantise_hidden(prior, 0, 0, BATCH, grouped_p0)
+        first_layer(post, 1, (0,), 0, BATCH)
+        turn_weight(post, 2, (3, 4), S)
         turn_second_weight(prior)
+        grouped_p1 = group_hidden(prior, 1, 0, BATCH)
+        first_layer(post, 1, (1,), 0, BATCH)
         turn_second_weight(post)
-        turn_unit(post, 2)
-        quantise_hidden(prior, 1, 0, BATCH, grouped_a)
-        first_layer(post, 1, 0, BATCH)
-
-        grouped_a = group_hidden(post, 0, 0, BATCH)
-        turn_unit(post, 3)
-        quantise_hidden(post, 0, 0, BATCH, grouped_a)
+        turn_weight(post, 3, range(2), S)
+        quantise_hidden(prior, 1, 0, BATCH, grouped_p1)
+        first_layer(post, 2, (0,), 0, BATCH)
+        turn_weight(post, 3, (2, 3, 4), S)
+        grouped_q0 = group_hidden(post, 0, 0, BATCH)
         prior_result = second_layer(prior, 0, ROW_TILES)
-        first_layer(post, 2, 0, BATCH)
-
-        first_layer(post, 3, 0, HALF)
+        first_layer(post, 2, (1,), 0, BATCH)
+        quantise_hidden(post, 0, 0, BATCH, grouped_q0)
+        first_layer(post, 3, both, 0, HALF)
         quantise_hidden(post, 1, 0, HALF, group_hidden(post, 1, 0, HALF))
-        first_layer(post, 3, HALF, HALF)
+        first_layer(post, 3, both, HALF, HALF)
         first_result = second_layer(post, 0, 2)
         quantise_hidden(post, 1, HALF, HALF, group_hidden(post, 1, HALF, HALF))
         second_result = second_layer(post, 2, 2)

@@ -45,10 +45,9 @@ def tile_rssmcell_pb_kernel(
         h_rows = keep.tile([P, ROW_TILES, DETER], BF16, name="h_rows")
         e_rows = keep.tile([P, ROW_TILES, EMBED], BF16, name="e_rows")
 
-        def load_batch_rows(rows, source):
+        def load_batch_rows(rows, source, half):
             view = source.rearrange("(p t) k -> p t k", t=ROW_TILES)
-            for half in range(2):
-                nc.sync.dma_start(out=rows[:, 2 * half : 2 * half + 2, :], in_=view[:, 2 * half : 2 * half + 2, :])
+            nc.sync.dma_start(out=rows[:, 2 * half : 2 * half + 2, :], in_=view[:, 2 * half : 2 * half + 2, :])
 
         def load_unit(head, unit):
             features = head["passes"] * K_PASS
@@ -62,9 +61,12 @@ def tile_rssmcell_pb_kernel(
             nc.scalar.dma_start(out=bias1_bf[:], in_=head["b1"].rearrange("(g p j) -> p g j", g=HID_PASSES, p=P, j=PACK))
             head["bias1_bf"] = bias1_bf
 
-        load_batch_rows(h_rows, h)
-        prior["rows"] = [load_unit(prior, unit) for unit in range(UNITS)]
-        load_batch_rows(e_rows, embedding)
+        load_batch_rows(h_rows, h, 0)
+        prior["rows"] = [load_unit(prior, 0)]
+        load_batch_rows(h_rows, h, 1)
+        prior["rows"].extend([load_unit(prior, unit) for unit in range(1, UNITS)])
+        for half in range(2):
+            load_batch_rows(e_rows, embedding, half)
         post["rows"] = [load_unit(post, unit) for unit in range(2)]
         for head in (prior, post):
             w2_rows = keep.tile([P, HID], BF16, name="%s_w2_rows" % head["name"])
@@ -227,12 +229,17 @@ def tile_rssmcell_pb_kernel(
             for part in ("v", "size", "decay", "mean", "hinge"):
                 head[part] = keep.tile([P, ROW_TILES, STOC], F32, name="%s_%s" % (head["name"], part))
 
-        def begin_softplus(head, first_tile, tiles, result):
+        def add_bias(head, first_tile, tiles, result):
+            nc.vector.tensor_tensor(
+                out=head["v"][:, first_tile : first_tile + tiles, :],
+                in0=result[:, :, STOC:DIST],
+                in1=spread_bias2(head, slice(STOC, DIST), tiles),
+                op=ALU.add,
+            )
+
+        def decay_of(head, first_tile, tiles):
             span = slice(first_tile, first_tile + tiles)
             v, size, decay = [head[part][:, span, :] for part in ("v", "size", "decay")]
-            nc.vector.tensor_tensor(
-                out=v, in0=result[:, :, STOC:DIST], in1=spread_bias2(head, slice(STOC, DIST), tiles), op=ALU.add
-            )
             nc.scalar.activation(out=size, in_=v, func=ACT.Abs)
             nc.scalar.activation(out=decay, in_=size, func=ACT.Exp, scale=-1.0)
 
@@ -254,13 +261,15 @@ def tile_rssmcell_pb_kernel(
             nc.sync.dma_start(out=by_partition(head["std_out"]), in_=std[:])
 
         both = (0, 1)
-        turn_batch_rows(h_rows, 0, H_PASSES, both)
+        turn_batch_rows(h_rows, 0, H_PASSES, (0,))
         for head in (prior, post):
             nc.vector.tensor_copy(out=head["bias1"][:], in_=head["bias1_bf"][:])
         S = nc.scalar.copy
         turn_weight(prior, 0, range(2), S)
+        turn_batch_rows(h_rows, 0, H_PASSES, (1,))
+        first_layer(prior, 0, both, 0, HALF)
         turn_weight(prior, 1, range(2), S)
-        first_layer(prior, 0, both, 0, BATCH)
+        first_layer(prior, 0, both, HALF, HALF)
         turn_weight(prior, 2, range(2), S)
         first_layer(prior, 1, both, 0, BATCH)
         turn_weight(prior, 3, range(2), S)
@@ -276,34 +285,42 @@ def tile_rssmcell_pb_kernel(
         first_layer(post, 0, (0,), 0, BATCH)
         turn_weight(post, 1, (3, 4), S)
         grouped_p0 = group_hidden(prior, 0, 0, BATCH)
-        first_layer(post, 0, (1,), 0, BATCH)
+        first_layer(post, 0, (1,), 0, BATCH, True)
         turn_weight(post, 2, range(3), S)
         quantise_hidden(prior, 0, 0, BATCH, grouped_p0)
         first_layer(post, 1, (0,), 0, BATCH)
         turn_weight(post, 2, (3, 4), S)
         turn_second_weight(prior)
         grouped_p1 = group_hidden(prior, 1, 0, BATCH)
-        first_layer(post, 1, (1,), 0, BATCH)
+        first_layer(post, 1, (1,), 0, BATCH, True)
         turn_second_weight(post)
         turn_weight(post, 3, range(2), S)
         quantise_hidden(prior, 1, 0, BATCH, grouped_p1)
         first_layer(post, 2, (0,), 0, BATCH)
-        turn_weight(post, 3, (2, 3, 4), S)
         grouped_q0 = group_hidden(post, 0, 0, BATCH)
+        turn_weight(post, 3, (2, 3, 4), S)
         prior_result = second_layer(prior, 0, ROW_TILES)
-        first_layer(post, 2, (1,), 0, BATCH)
+        first_layer(post, 2, (1,), 0, BATCH, True)
         quantise_hidden(post, 0, 0, BATCH, grouped_q0)
+        add_bias(prior, 0, ROW_TILES, prior_result)
+        decay_of(prior, 0, ROW_TILES)
+        mean_and_hinge(prior, 0, ROW_TILES, prior_result)
         first_layer(post, 3, both, 0, HALF)
         quantise_hidden(post, 1, 0, HALF, group_hidden(post, 1, 0, HALF))
-        first_layer(post, 3, both, HALF, HALF)
+        first_layer(post, 3, both, 2 * P, P, True)
+        quantise_hidden(post, 1, 2 * P, P, group_hidden(post, 1, 2 * P, P))
+        first_layer(post, 3, both, 3 * P, P, True)
         first_result = second_layer(post, 0, 2)
-        quantise_hidden(post, 1, HALF, HALF, group_hidden(post, 1, HALF, HALF))
-        second_result = second_layer(post, 2, 2)
-        begin_softplus(prior, 0, ROW_TILES, prior_result)
-        begin_softplus(post, 0, 2, first_result)
-        begin_softplus(post, 2, 2, second_result)
-        mean_and_hinge(prior, 0, ROW_TILES, prior_result)
+        quantise_hidden(post, 1, 3 * P, P, group_hidden(post, 1, 3 * P, P))
+        second_result = second_layer(post, 2, 1)
+        third_result = second_layer(post, 3, 1)
+        add_bias(post, 0, 2, first_result)
+        decay_of(post, 0, 2)
+        add_bias(post, 2, 1, second_result)
+        add_bias(post, 3, 1, third_result)
+        decay_of(post, 2, 2)
         mean_and_hinge(post, 0, 2, first_result)
-        mean_and_hinge(post, 2, 2, second_result)
+        mean_and_hinge(post, 2, 1, second_result)
+        mean_and_hinge(post, 3, 1, third_result)
         finish_outputs(post)
         finish_outputs(prior)

@@ -84,6 +84,14 @@ def tile_rssmcell_pb_kernel(
         nc.vector.memset(zero[:], 0.0)
         nc.scalar.activation(out=one[:], in_=zero[:], func=ACT.Exp)
 
+        still = keep.tile([P, 4 * P], BF16, name="still")
+        nc.vector.memset(still[:], 0.0)
+        unread = sums.tile([P, 4 * P], F32, name="total")
+
+        def keep_clock(times):
+            for repeat in range(times):
+                nc.tensor.matmul(unread[:], lhsT=still[:, 0:P], rhs=still[:], start=True, stop=True)
+
         def turn_bank(blocks):
             bank = turned.tile([P, 2, 2, P], F32, name="bank")
             for i in range(2):
@@ -261,12 +269,16 @@ def tile_rssmcell_pb_kernel(
             nc.sync.dma_start(out=by_partition(head["std_out"]), in_=std[:])
 
         both = (0, 1)
+        keep_clock(6)
         turn_batch_rows(h_rows, 0, H_PASSES, (0,))
+        keep_clock(1)
         for head in (prior, post):
             nc.vector.tensor_copy(out=head["bias1"][:], in_=head["bias1_bf"][:])
         S = nc.scalar.copy
         turn_weight(prior, 0, range(2), S)
+        keep_clock(2)
         turn_batch_rows(h_rows, 0, H_PASSES, (1,))
+        keep_clock(1)
         first_layer(prior, 0, both, 0, HALF)
         turn_weight(prior, 1, range(2), S)
         first_layer(prior, 0, both, HALF, HALF)

@@ -56,10 +56,16 @@ def tile_rssmcell_pb_kernel(
             nc.sync.dma_start(out=rows[:], in_=view[unit // 2, unit % 2])
             return rows
 
+        bias1_rows = keep.tile([P, K_PASS], BF16, name="bias1_rows")
+        bias2_row = keep.tile([P, 2, DIST], BF16, name="bias2_row")
+        nc.vector.memset(bias1_rows[:], 0.0)
+        nc.vector.memset(bias2_row[:], 0.0)
         for head in (prior, post):
-            bias1_bf = keep.tile([P, HID_PASSES, PACK], BF16, name="%s_bias1_bf" % head["name"])
-            nc.scalar.dma_start(out=bias1_bf[:], in_=head["b1"].rearrange("(g p j) -> p g j", g=HID_PASSES, p=P, j=PACK))
-            head["bias1_bf"] = bias1_bf
+            first = HID_PASSES * head["slot"]
+            nc.scalar.dma_start(
+                out=bias1_rows[first : first + HID_PASSES, :], in_=head["b1"].rearrange("(g k) -> g k", g=HID_PASSES)
+            )
+            nc.scalar.dma_start(out=bias2_row[0:1, head["slot"], :], in_=head["b2"].unsqueeze(0))
 
         load_batch_rows(h_rows, h, 0)
         prior["rows"] = [load_unit(prior, 0)]
@@ -73,12 +79,13 @@ def tile_rssmcell_pb_kernel(
             nc.sync.dma_start(out=w2_rows[:], in_=head["w2"])
             head["w2_rows"] = w2_rows
         post["rows"].extend([load_unit(post, unit) for unit in range(2, UNITS)])
-        bias2 = keep.tile([P, 2, DIST], BF16, name="bias2")
-        for head in (prior, post):
-            nc.sync.dma_start(out=bias2[:, head["slot"], :], in_=head["b2"].partition_broadcast(P))
 
         ident = keep.tile([P, P], F32, name="ident")
         make_identity(nc, ident[:])
+        ident_bf = keep.tile([P, P], BF16, name="ident_bf")
+        nc.vector.tensor_copy(out=ident_bf[:], in_=ident[:])
+        ones = keep.tile([P, P], BF16, name="ones")
+        nc.vector.memset(ones[:], 1.0)
         zero = keep.tile([P, 1], F32, name="zero")
         one = keep.tile([P, 1], F32, name="one")
         nc.vector.memset(zero[:], 0.0)
@@ -163,7 +170,6 @@ def tile_rssmcell_pb_kernel(
 
         for head in (prior, post):
             head["codes"], head["scales"] = {}, {}
-            head["bias1"] = keep.tile([P, HID_PASSES, PACK], F32, name="%s_bias1" % head["name"])
             head["hidden"] = [
                 keep.tile([P, PACK, BATCH], BF16, name="%s_hidden%d" % (head["name"], g)) for g in range(HID_PASSES)
             ]
@@ -187,7 +193,7 @@ def tile_rssmcell_pb_kernel(
                         stop=(g == passes - 1),
                     )
                 j = 2 * (unit % 2) + i
-                bias = head["bias1"][:, unit // 2, j : j + 1]
+                bias = bias1[:, HID_PASSES * head["slot"] + unit // 2, j : j + 1]
                 rounded = head["hidden"][unit // 2][:, j, columns]
                 if i == 0 or alone:
                     nc.scalar.activation(out=rounded, in_=total[:], func=ACT.Relu, bias=bias, scale=1.0)
@@ -237,6 +243,27 @@ def tile_rssmcell_pb_kernel(
             for part in ("v", "size", "decay", "mean", "hinge"):
                 head[part] = keep.tile([P, ROW_TILES, STOC], F32, name="%s_%s" % (head["name"], part))
 
+        bias1 = keep.tile([P, 2 * HID_PASSES, PACK], F32, name="bias1")
+        bias2 = keep.tile([P, 2, DIST], F32, name="bias2")
+
+        def spread_biases():
+            columns = bias1_rows[:].rearrange("r (p j) -> r j p", j=PACK)
+            turned_rows = turned.tile([P, PACK, P], BF16, name="bank")
+            for j in range(PACK):
+                nc.tensor.transpose(turned_rows[:, j, :], columns[:, j, :], ident_bf[:])
+            nc.vector.tensor_copy(
+                out=bias1[:], in_=turned_rows[:, :, 0 : 2 * HID_PASSES].rearrange("p j r -> p r j")
+            )
+            spread = turned.tile([P, 2, DIST], F32, name="bank")
+            nc.tensor.matmul(
+                spread[:].rearrange("p s d -> p (s d)"),
+                lhsT=ones[:],
+                rhs=bias2_row[:].rearrange("p s d -> p (s d)"),
+                start=True,
+                stop=True,
+            )
+            nc.vector.tensor_copy(out=bias2[:], in_=spread[:])
+
         def add_bias(head, first_tile, tiles, result):
             nc.vector.tensor_tensor(
                 out=head["v"][:, first_tile : first_tile + tiles, :],
@@ -272,11 +299,10 @@ def tile_rssmcell_pb_kernel(
         keep_clock(6)
         turn_batch_rows(h_rows, 0, H_PASSES, (0,))
         keep_clock(1)
-        for head in (prior, post):
-            nc.vector.tensor_copy(out=head["bias1"][:], in_=head["bias1_bf"][:])
         S = nc.scalar.copy
         turn_weight(prior, 0, range(2), S)
-        keep_clock(2)
+        spread_biases()
+        keep_clock(1)
         turn_batch_rows(h_rows, 0, H_PASSES, (1,))
         keep_clock(1)
         first_layer(prior, 0, both, 0, HALF)

@@ -42,6 +42,23 @@ def tile_rssmcell_pb_kernel(
         prior = dict(name="prior", slot=0, passes=H_PASSES, w1=wp1, b1=bp1, w2=wp2, b2=bp2, mean_out=prior_mean, std_out=prior_std)
         post = dict(name="post", slot=1, passes=C_PASSES, w1=wq1, b1=bq1, w2=wq2, b2=bq2, mean_out=post_mean, std_out=post_std)
 
+        ident = keep.tile([P, P], F32, name="ident")
+        make_identity(nc, ident[:])
+        zero = keep.tile([P, 1], F32, name="zero")
+        one = keep.tile([P, 1], F32, name="one")
+        nc.vector.memset(zero[:], 0.0)
+        nc.scalar.activation(out=one[:], in_=zero[:], func=ACT.Exp)
+
+        still = keep.tile([P, 4 * P], BF16, name="still")
+        nc.vector.memset(still[:], 0.0)
+        ones = keep.tile([P, P], BF16, name="ones")
+        nc.vector.memset(ones[:], 1.0)
+        unread = sums.tile([P, 4 * P], F32, name="total")
+
+        def keep_clock(times):
+            for repeat in range(times):
+                nc.tensor.matmul(unread[:], lhsT=still[:, 0:P], rhs=still[:], start=True, stop=True)
+
         h_rows = keep.tile([P, ROW_TILES, DETER], BF16, name="h_rows")
         e_rows = keep.tile([P, ROW_TILES, EMBED], BF16, name="e_rows")
 
@@ -52,10 +69,12 @@ def tile_rssmcell_pb_kernel(
         def load_unit(head, unit):
             features = head["passes"] * K_PASS
             rows = keep.tile([P, 2, features], BF16, name="%s_rows%d" % (head["name"], unit))
-            view = head["w1"].rearrange("(g p c i) k -> g c p i k", g=HID_PASSES, p=P, c=2, i=2)
+            view = head["w1"].rearrange("(g c p i) k -> g c p i k", g=HID_PASSES, c=2, p=P, i=2)
             nc.sync.dma_start(out=rows[:], in_=view[unit // 2, unit % 2])
             return rows
 
+        load_batch_rows(h_rows, h, 0)
+        prior["rows"] = [load_unit(prior, 0)]
         bias1_rows = keep.tile([P, K_PASS], BF16, name="bias1_rows")
         bias2_row = keep.tile([P, 2, DIST], BF16, name="bias2_row")
         nc.vector.memset(bias1_rows[:], 0.0)
@@ -66,9 +85,9 @@ def tile_rssmcell_pb_kernel(
                 out=bias1_rows[first : first + HID_PASSES, :], in_=head["b1"].rearrange("(g k) -> g k", g=HID_PASSES)
             )
             nc.scalar.dma_start(out=bias2_row[0:1, head["slot"], :], in_=head["b2"].unsqueeze(0))
+        ident_bf = keep.tile([P, P], BF16, name="ident_bf")
+        nc.vector.tensor_copy(out=ident_bf[:], in_=ident[:])
 
-        load_batch_rows(h_rows, h, 0)
-        prior["rows"] = [load_unit(prior, 0)]
         load_batch_rows(h_rows, h, 1)
         prior["rows"].extend([load_unit(prior, unit) for unit in range(1, UNITS)])
         for half in range(2):
@@ -79,25 +98,6 @@ def tile_rssmcell_pb_kernel(
             nc.sync.dma_start(out=w2_rows[:], in_=head["w2"])
             head["w2_rows"] = w2_rows
         post["rows"].extend([load_unit(post, unit) for unit in range(2, UNITS)])
-
-        ident = keep.tile([P, P], F32, name="ident")
-        make_identity(nc, ident[:])
-        ident_bf = keep.tile([P, P], BF16, name="ident_bf")
-        nc.vector.tensor_copy(out=ident_bf[:], in_=ident[:])
-        ones = keep.tile([P, P], BF16, name="ones")
-        nc.vector.memset(ones[:], 1.0)
-        zero = keep.tile([P, 1], F32, name="zero")
-        one = keep.tile([P, 1], F32, name="one")
-        nc.vector.memset(zero[:], 0.0)
-        nc.scalar.activation(out=one[:], in_=zero[:], func=ACT.Exp)
-
-        still = keep.tile([P, 4 * P], BF16, name="still")
-        nc.vector.memset(still[:], 0.0)
-        unread = sums.tile([P, 4 * P], F32, name="total")
-
-        def keep_clock(times):
-            for repeat in range(times):
-                nc.tensor.matmul(unread[:], lhsT=still[:, 0:P], rhs=still[:], start=True, stop=True)
 
         def turn_bank(blocks):
             bank = turned.tile([P, 2, 2, P], F32, name="bank")
@@ -118,65 +118,74 @@ def tile_rssmcell_pb_kernel(
         c_codes = keep.tile([P, C_PASSES, BATCH], U32, name="c_codes", align_bytes=64)
         c_scales = keep.tile([P, C_PASSES, BATCH], U8, name="c_scales", align_bytes=64)
 
-        def turn_batch_rows(rows, first_pass, passes, halves):
+        def turn_batch_rows(rows, first_pass, passes, half, copies):
             words = rows[:].bitcast(F32)
-            for half in halves:
-                tiles = slice(2 * half, 2 * half + 2)
-                grouped = []
-                for g in range(passes):
-                    bank = turn_bank(pass_blocks(words[:, tiles, :], g))
-                    grouped_c = ring.tile([P, 2, P, PACK], BF16, name="grouped_w", bufs=10, align_bytes=64)
-                    grouped.append(grouped_c)
-                    engine_copy = nc.scalar.copy if (half * passes + g) % 2 == 0 else nc.vector.tensor_copy
-                    copy_bank(engine_copy, bank, grouped_c[:].bitcast(F32))
-                for g in range(passes):
-                    nc.vector.quantize_mx(
-                        out=c_codes[:, first_pass + g, HALF * half : HALF * half + HALF].bitcast(FP8X4),
-                        scales=c_scales[:, first_pass + g, HALF * half : HALF * half + HALF],
-                        in_=grouped[g][:].rearrange("p t r j -> p (t r j)"),
-                    )
+            waiting = []
+            for g in range(passes):
+                bank = turn_bank(pass_blocks(words[:, 2 * half : 2 * half + 2, :], g))
+                grouped_c = ring.tile([P, 2, P, PACK], BF16, name="grouped_w", bufs=12, align_bytes=64)
+                copy_bank(copies[g], bank, grouped_c[:].bitcast(F32))
+                waiting.append((first_pass + g, half, grouped_c))
+            return waiting
 
-        def turn_weight(head, unit, pieces, engine_copy):
-            passes = head["passes"]
-            words = head["rows"][unit][:].bitcast(F32)
-            if unit not in head["codes"]:
-                head["codes"][unit] = keep.tile([P, passes, 2 * P], U32, name="%s_codes%d" % (head["name"], unit), align_bytes=64)
-                head["scales"][unit] = keep.tile([P, passes, 2 * P], U8, name="%s_scales%d" % (head["name"], unit), align_bytes=64)
-            codes, scales = head["codes"][unit], head["scales"][unit]
-            for g in pieces:
-                bank = turn_bank(pass_blocks(words, g))
-                grouped_w = ring.tile([P, 2, P, PACK], BF16, name="grouped_w", bufs=10, align_bytes=64)
-                copy_bank(engine_copy, bank, grouped_w[:].bitcast(F32))
+        def quantise_batch_rows(waiting):
+            for g, half, grouped_c in waiting:
                 nc.vector.quantize_mx(
-                    out=codes[:, g, :].bitcast(FP8X4),
-                    scales=scales[:, g, :],
+                    out=c_codes[:, g, HALF * half : HALF * half + HALF].bitcast(FP8X4),
+                    scales=c_scales[:, g, HALF * half : HALF * half + HALF],
+                    in_=grouped_c[:].rearrange("p t r j -> p (t r j)"),
+                )
+
+        def turn_weight(head, unit, pieces, copies):
+            words = head["rows"][unit][:].bitcast(F32)
+            waiting = []
+            for g, engine_copy in zip(pieces, copies):
+                bank = turn_bank(pass_blocks(words, g))
+                grouped_w = ring.tile([P, 2, P, PACK], BF16, name="grouped_w", bufs=12, align_bytes=64)
+                copy_bank(engine_copy, bank, grouped_w[:].bitcast(F32))
+                waiting.append((head, unit, g, grouped_w))
+            return waiting
+
+        def quantise_weight(waiting):
+            for head, unit, g, grouped_w in waiting:
+                nc.vector.quantize_mx(
+                    out=head["codes"][unit][:, g, :].bitcast(FP8X4),
+                    scales=head["scales"][unit][:, g, :],
                     in_=grouped_w[:].rearrange("p i r j -> p (i r j)"),
                 )
 
         def turn_second_weight(head):
-            words = head["w2_rows"][:].bitcast(F32).rearrange("d (g p u) -> d g u p", g=HID_PASSES, p=P, u=2)
+            words = head["w2_rows"][:].bitcast(F32).rearrange("d (g u p) -> d g u p", g=HID_PASSES, u=2, p=P)
             bank = turn_bank([[words[:, g, u, :] for u in range(2)] for g in range(HID_PASSES)])
-            grouped_w = ring.tile([P, 2, P, PACK], BF16, name="grouped_w", bufs=10, align_bytes=64)
+            grouped_w = ring.tile([P, 2, P, PACK], BF16, name="grouped_w", bufs=12, align_bytes=64)
             copy_bank(nc.scalar.copy, bank, grouped_w[:].bitcast(F32))
-            codes = keep.tile([P, HID_PASSES, DIST], U32, name="%s_w2_codes" % head["name"], align_bytes=64)
-            scales = keep.tile([P, HID_PASSES, DIST], U8, name="%s_w2_scales" % head["name"], align_bytes=64)
+            return grouped_w
+
+        def quantise_second_weight(head, grouped_w):
+            head["w2_codes"] = keep.tile([P, HID_PASSES, DIST], U32, name="%s_w2_codes" % head["name"], align_bytes=64)
+            head["w2_scales"] = keep.tile([P, HID_PASSES, DIST], U8, name="%s_w2_scales" % head["name"], align_bytes=64)
             nc.vector.quantize_mx(
-                out=codes[:].rearrange("p g d -> p (g d)").bitcast(FP8X4),
-                scales=scales[:].rearrange("p g d -> p (g d)"),
+                out=head["w2_codes"][:].rearrange("p g d -> p (g d)").bitcast(FP8X4),
+                scales=head["w2_scales"][:].rearrange("p g d -> p (g d)"),
                 in_=grouped_w[:].rearrange("p g d j -> p (g d j)"),
             )
-            head["w2_codes"] = codes
-            head["w2_scales"] = scales
 
         for head in (prior, post):
-            head["codes"], head["scales"] = {}, {}
+            shape = [P, head["passes"], 2 * P]
+            head["codes"] = [
+                keep.tile(shape, U32, name="%s_codes%d" % (head["name"], unit), align_bytes=64) for unit in range(UNITS)
+            ]
+            head["scales"] = [
+                keep.tile(shape, U8, name="%s_scales%d" % (head["name"], unit), align_bytes=64) for unit in range(UNITS)
+            ]
             head["hidden"] = [
                 keep.tile([P, PACK, BATCH], BF16, name="%s_hidden%d" % (head["name"], g)) for g in range(HID_PASSES)
             ]
             head["a_codes"] = keep.tile([P, HID_PASSES, BATCH], U32, name="%s_a_codes" % head["name"], align_bytes=64)
             head["a_scales"] = keep.tile([P, HID_PASSES, BATCH], U8, name="%s_a_scales" % head["name"], align_bytes=64)
 
-        def first_layer(head, unit, tiles, first, width, alone=False):
+        def first_layer(head, unit, tiles, first, width):
+            waiting = []
             passes = head["passes"]
             codes, scales = head["codes"][unit], head["scales"][unit]
             columns = slice(first, first + width)
@@ -192,10 +201,15 @@ def tile_rssmcell_pb_kernel(
                         start=(g == 0),
                         stop=(g == passes - 1),
                     )
+                waiting.append((head, unit, i, columns, total))
+            return waiting
+
+        def empty_sums(waiting, on_scalar):
+            for head, unit, i, columns, total in waiting:
                 j = 2 * (unit % 2) + i
                 bias = bias1[:, HID_PASSES * head["slot"] + unit // 2, j : j + 1]
                 rounded = head["hidden"][unit // 2][:, j, columns]
-                if i == 0 or alone:
+                if on_scalar:
                     nc.scalar.activation(out=rounded, in_=total[:], func=ACT.Relu, bias=bias, scale=1.0)
                 else:
                     nc.vector.tensor_scalar(
@@ -203,7 +217,7 @@ def tile_rssmcell_pb_kernel(
                     )
 
         def group_hidden(head, g, first, width):
-            grouped_a = ring.tile([P, width, PACK], BF16, name="grouped_a", bufs=2, align_bytes=64)
+            grouped_a = ring.tile([P, width, PACK], BF16, name="grouped_a", bufs=3, align_bytes=64)
             nc.vector.tensor_copy(
                 out=grouped_a[:].rearrange("p (c i) j -> p c j i", i=4),
                 in_=head["hidden"][g][:, :, first : first + width].rearrange("p j (c i) -> p c j i", i=4),
@@ -247,10 +261,10 @@ def tile_rssmcell_pb_kernel(
         bias2 = keep.tile([P, 2, DIST], F32, name="bias2")
 
         def spread_biases():
-            columns = bias1_rows[:].rearrange("r (p j) -> r j p", j=PACK)
+            columns = bias1_rows[:].rearrange("r (c p i) -> r c i p", c=2, i=2)
             turned_rows = turned.tile([P, PACK, P], BF16, name="bank")
             for j in range(PACK):
-                nc.tensor.transpose(turned_rows[:, j, :], columns[:, j, :], ident_bf[:])
+                nc.tensor.transpose(turned_rows[:, j, :], columns[:, j // 2, j % 2, :], ident_bf[:])
             nc.vector.tensor_copy(
                 out=bias1[:], in_=turned_rows[:, :, 0 : 2 * HID_PASSES].rearrange("p j r -> p r j")
             )
@@ -271,6 +285,12 @@ def tile_rssmcell_pb_kernel(
                 in1=spread_bias2(head, slice(STOC, DIST), tiles),
                 op=ALU.add,
             )
+
+        def last_decay_of(head, first_tile, tiles):
+            span = slice(first_tile, first_tile + tiles)
+            v, size, decay = [head[part][:, span, :] for part in ("v", "size", "decay")]
+            nc.vector.scalar_tensor_tensor(out=size, in0=v, scalar=-1.0, in1=v, op0=ALU.mult, op1=ALU.min)
+            nc.scalar.activation(out=decay, in_=size, func=ACT.Exp)
 
         def decay_of(head, first_tile, tiles):
             span = slice(first_tile, first_tile + tiles)
@@ -296,67 +316,109 @@ def tile_rssmcell_pb_kernel(
             nc.sync.dma_start(out=by_partition(head["std_out"]), in_=std[:])
 
         both = (0, 1)
+        S, V = nc.scalar.copy, nc.vector.tensor_copy
         keep_clock(6)
-        turn_batch_rows(h_rows, 0, H_PASSES, (0,))
+        h0 = turn_batch_rows(h_rows, 0, H_PASSES, 0, (S, V))
         keep_clock(1)
-        S = nc.scalar.copy
-        turn_weight(prior, 0, range(2), S)
+        quantise_batch_rows(h0)
+        p0 = turn_weight(prior, 0, range(2), (S, V))
         spread_biases()
         keep_clock(1)
-        turn_batch_rows(h_rows, 0, H_PASSES, (1,))
+        quantise_weight(p0)
+        h1 = turn_batch_rows(h_rows, 0, H_PASSES, 1, (S, V))
         keep_clock(1)
-        first_layer(prior, 0, both, 0, HALF)
-        turn_weight(prior, 1, range(2), S)
-        first_layer(prior, 0, both, HALF, HALF)
-        turn_weight(prior, 2, range(2), S)
-        first_layer(prior, 1, both, 0, BATCH)
-        turn_weight(prior, 3, range(2), S)
-        first_layer(prior, 2, (0,), 0, BATCH)
-        turn_batch_rows(e_rows, H_PASSES, C_PASSES - H_PASSES, (0,))
-        first_layer(prior, 2, (1,), 0, BATCH)
-        turn_batch_rows(e_rows, H_PASSES, C_PASSES - H_PASSES, (1,))
-        first_layer(prior, 3, (0,), 0, BATCH)
-        turn_weight(post, 0, range(3), S)
-        first_layer(prior, 3, (1,), 0, BATCH)
-        turn_weight(post, 0, (3, 4), S)
-        turn_weight(post, 1, range(3), S)
-        first_layer(post, 0, (0,), 0, BATCH)
-        turn_weight(post, 1, (3, 4), S)
+        m0 = first_layer(prior, 0, both, 0, HALF)
+        quantise_batch_rows(h1)
+        empty_sums(m0[:1], True)
+        empty_sums(m0[1:], False)
+        p1 = turn_weight(prior, 1, range(2), (S, V))
+        m0 = first_layer(prior, 0, both, HALF, HALF)
+        quantise_weight(p1)
+        empty_sums(m0[:1], True)
+        empty_sums(m0[1:], False)
+        p2 = turn_weight(prior, 2, range(2), 3 * (S,))
+        m1 = first_layer(prior, 1, both, 0, BATCH)
+        quantise_weight(p2)
+        empty_sums(m1[:1], True)
+        empty_sums(m1[1:], False)
+        p3 = turn_weight(prior, 3, range(2), 3 * (S,))
+        quantise_weight(p3)
+        m2 = first_layer(prior, 2, (0,), 0, BATCH)
+        empty_sums(m2, True)
+        e0 = turn_batch_rows(e_rows, H_PASSES, C_PASSES - H_PASSES, 0, (S, V, S))
+        quantise_batch_rows(e0)
+        m3 = first_layer(prior, 2, (1,), 0, BATCH)
+        empty_sums(m3, True)
+        e1 = turn_batch_rows(e_rows, H_PASSES, C_PASSES - H_PASSES, 1, (V, S, S))
+        quantise_batch_rows(e1)
+        m2 = first_layer(prior, 3, (0,), 0, BATCH)
+        empty_sums(m2, False)
+        q0a = turn_weight(post, 0, range(3), 3 * (S,))
+        quantise_weight(q0a)
+        m3 = first_layer(prior, 3, (1,), 0, BATCH)
+        empty_sums(m3, False)
+        q0b = turn_weight(post, 0, (3, 4), 3 * (S,))
+        quantise_weight(q0b)
+        q1a = turn_weight(post, 1, range(3), 3 * (S,))
+        quantise_weight(q1a)
+        m2 = first_layer(post, 0, (0,), 0, BATCH)
+        empty_sums(m2, True)
+        q1b = turn_weight(post, 1, (3, 4), 3 * (S,))
         grouped_p0 = group_hidden(prior, 0, 0, BATCH)
-        first_layer(post, 0, (1,), 0, BATCH, True)
-        turn_weight(post, 2, range(3), S)
+        quantise_weight(q1b)
+        m3 = first_layer(post, 0, (1,), 0, BATCH)
+        empty_sums(m3, True)
+        q2a = turn_weight(post, 2, range(3), 3 * (S,))
         quantise_hidden(prior, 0, 0, BATCH, grouped_p0)
-        first_layer(post, 1, (0,), 0, BATCH)
-        turn_weight(post, 2, (3, 4), S)
-        turn_second_weight(prior)
+        quantise_weight(q2a)
+        m2 = first_layer(post, 1, (0,), 0, BATCH)
+        empty_sums(m2, True)
+        q2b = turn_weight(post, 2, (3, 4), 3 * (S,))
+        w2p = turn_second_weight(prior)
         grouped_p1 = group_hidden(prior, 1, 0, BATCH)
-        first_layer(post, 1, (1,), 0, BATCH, True)
-        turn_second_weight(post)
-        turn_weight(post, 3, range(2), S)
+        quantise_weight(q2b)
+        quantise_second_weight(prior, w2p)
+        m3 = first_layer(post, 1, (1,), 0, BATCH)
+        empty_sums(m3, True)
+        w2q = turn_second_weight(post)
+        q3a = turn_weight(post, 3, range(2), 3 * (S,))
         quantise_hidden(prior, 1, 0, BATCH, grouped_p1)
-        first_layer(post, 2, (0,), 0, BATCH)
+        quantise_second_weight(post, w2q)
+        m2 = first_layer(post, 2, (0,), 0, BATCH)
+        empty_sums(m2, True)
+        quantise_weight(q3a)
         grouped_q0 = group_hidden(post, 0, 0, BATCH)
-        turn_weight(post, 3, (2, 3, 4), S)
+        q3b = turn_weight(post, 3, (2, 3, 4), 3 * (S,))
         prior_result = second_layer(prior, 0, ROW_TILES)
-        first_layer(post, 2, (1,), 0, BATCH, True)
+        m3 = first_layer(post, 2, (1,), 0, BATCH)
+        quantise_weight(q3b)
         quantise_hidden(post, 0, 0, BATCH, grouped_q0)
         add_bias(prior, 0, ROW_TILES, prior_result)
-        decay_of(prior, 0, ROW_TILES)
         mean_and_hinge(prior, 0, ROW_TILES, prior_result)
-        first_layer(post, 3, both, 0, HALF)
-        quantise_hidden(post, 1, 0, HALF, group_hidden(post, 1, 0, HALF))
-        first_layer(post, 3, both, 2 * P, P, True)
-        quantise_hidden(post, 1, 2 * P, P, group_hidden(post, 1, 2 * P, P))
-        first_layer(post, 3, both, 3 * P, P, True)
+        empty_sums(m3, True)
+        m4 = first_layer(post, 3, both, 0, HALF)
+        empty_sums(m4[:1], True)
+        empty_sums(m4[1:], False)
+        decay_of(prior, 0, ROW_TILES)
+        m5 = first_layer(post, 3, both, 2 * P, P)
+        grouped_a = group_hidden(post, 1, 0, HALF)
+        empty_sums(m5, True)
+        m6 = first_layer(post, 3, both, 3 * P, P)
+        empty_sums(m6, True)
+        grouped_b = group_hidden(post, 1, 2 * P, P)
+        quantise_hidden(post, 1, 0, HALF, grouped_a)
+        grouped_c = group_hidden(post, 1, 3 * P, P)
+        quantise_hidden(post, 1, 2 * P, P, grouped_b)
         first_result = second_layer(post, 0, 2)
-        quantise_hidden(post, 1, 3 * P, P, group_hidden(post, 1, 3 * P, P))
+        quantise_hidden(post, 1, 3 * P, P, grouped_c)
         second_result = second_layer(post, 2, 1)
         third_result = second_layer(post, 3, 1)
         add_bias(post, 0, 2, first_result)
         decay_of(post, 0, 2)
         add_bias(post, 2, 1, second_result)
+        decay_of(post, 2, 1)
         add_bias(post, 3, 1, third_result)
-        decay_of(post, 2, 2)
+        last_decay_of(post, 3, 1)
         mean_and_hinge(post, 0, 2, first_result)
         mean_and_hinge(post, 2, 1, second_result)
         mean_and_hinge(post, 3, 1, third_result)

@@ -92,12 +92,12 @@ def tile_rssmcell_pb_kernel(
         prior["rows"].extend([load_unit(prior, unit) for unit in range(1, UNITS)])
         for half in range(2):
             load_batch_rows(e_rows, embedding, half)
-        post["rows"] = [load_unit(post, unit) for unit in range(2)]
+        post["rows"] = [load_unit(post, unit) for unit in range(3)]
         for head in (prior, post):
             w2_rows = keep.tile([P, HID], BF16, name="%s_w2_rows" % head["name"])
             nc.sync.dma_start(out=w2_rows[:], in_=head["w2"])
             head["w2_rows"] = w2_rows
-        post["rows"].extend([load_unit(post, unit) for unit in range(2, UNITS)])
+        post["rows"].append(load_unit(post, 3))
 
         def turn_bank(blocks):
             bank = turned.tile([P, 2, 2, P], F32, name="bank")
@@ -184,14 +184,17 @@ def tile_rssmcell_pb_kernel(
             head["a_codes"] = keep.tile([P, HID_PASSES, BATCH], U32, name="%s_a_codes" % head["name"], align_bytes=64)
             head["a_scales"] = keep.tile([P, HID_PASSES, BATCH], U8, name="%s_a_scales" % head["name"], align_bytes=64)
 
-        def first_layer(head, unit, tiles, first, width):
+        def open_sums(head, unit, tiles, first, width):
             waiting = []
-            passes = head["passes"]
-            codes, scales = head["codes"][unit], head["scales"][unit]
-            columns = slice(first, first + width)
             for i in tiles:
                 total = sums.tile([P, width], F32, name="total")
-                for g in range(passes):
+                waiting.append((head, unit, i, slice(first, first + width), total))
+            return waiting
+
+        def add_passes(waiting, pieces):
+            for head, unit, i, columns, total in waiting:
+                codes, scales = head["codes"][unit], head["scales"][unit]
+                for g in pieces:
                     nc.tensor.matmul_mx(
                         out=total[:],
                         lhsT=codes[:, g, P * i : P * i + P].bitcast(FP8X4),
@@ -199,9 +202,15 @@ def tile_rssmcell_pb_kernel(
                         rhs=c_codes[:, g, columns].bitcast(FP8X4),
                         rhs_scale=c_scales[:, g, columns],
                         start=(g == 0),
-                        stop=(g == passes - 1),
+                        stop=(g == head["passes"] - 1),
                     )
-                waiting.append((head, unit, i, columns, total))
+
+        def first_layer(head, unit, tiles, first, width):
+            waiting = []
+            for i in tiles:
+                one = open_sums(head, unit, (i,), first, width)
+                add_passes(one, range(head["passes"]))
+                waiting.extend(one)
             return waiting
 
         def empty_sums(waiting, on_scalar):
@@ -358,15 +367,18 @@ def tile_rssmcell_pb_kernel(
         m3 = first_layer(prior, 3, (1,), 0, BATCH)
         empty_sums(m3, False)
         q0b = turn_weight(post, 0, (3, 4), 3 * (S,))
+        n0 = open_sums(post, 0, both, 0, BATCH)
+        add_passes(n0, range(H_PASSES))
         quantise_weight(q0b)
         q1a = turn_weight(post, 1, range(3), 3 * (S,))
         quantise_weight(q1a)
-        m2 = first_layer(post, 0, (0,), 0, BATCH)
-        empty_sums(m2, True)
+        add_passes(n0[:1], range(H_PASSES, C_PASSES))
+        empty_sums(n0[:1], True)
         q1b = turn_weight(post, 1, (3, 4), 3 * (S,))
         grouped_p0 = group_hidden(prior, 0, 0, BATCH)
         quantise_weight(q1b)
-        m3 = first_layer(post, 0, (1,), 0, BATCH)
+        add_passes(n0[1:], range(H_PASSES, C_PASSES))
+        m3 = n0[1:]
         empty_sums(m3, True)
         q2a = turn_weight(post, 2, range(3), 3 * (S,))
         quantise_hidden(prior, 0, 0, BATCH, grouped_p0)
@@ -374,15 +386,15 @@ def tile_rssmcell_pb_kernel(
         m2 = first_layer(post, 1, (0,), 0, BATCH)
         empty_sums(m2, True)
         q2b = turn_weight(post, 2, (3, 4), 3 * (S,))
-        w2p = turn_second_weight(prior)
         grouped_p1 = group_hidden(prior, 1, 0, BATCH)
         quantise_weight(q2b)
-        quantise_second_weight(prior, w2p)
         m3 = first_layer(post, 1, (1,), 0, BATCH)
         empty_sums(m3, True)
+        w2p = turn_second_weight(prior)
         w2q = turn_second_weight(post)
         q3a = turn_weight(post, 3, range(2), 3 * (S,))
         quantise_hidden(prior, 1, 0, BATCH, grouped_p1)
+        quantise_second_weight(prior, w2p)
         quantise_second_weight(post, w2q)
         m2 = first_layer(post, 2, (0,), 0, BATCH)
         empty_sums(m2, True)

from contextlib import ExitStack

import concourse.mybir as mybir
from concourse.masks import make_identity

F32 = mybir.dt.float32
BF16 = mybir.dt.bfloat16
U32 = mybir.dt.uint32
U8 = mybir.dt.uint8
FP8X4 = mybir.dt.float8_e4m3fn_x4
ACT = mybir.ActivationFunctionType
ALU = mybir.AluOpType

P = 128
PACK = 4
K_PASS = P * PACK
PASS_WORDS = K_PASS // 2

BATCH, DETER, EMBED, HID, DIST = 512, 1024, 1536, 1024, 128
STOC = DIST // 2
ROW_TILES = BATCH // P
H_PASSES = DETER // K_PASS
C_PASSES = (DETER + EMBED) // K_PASS
HID_PASSES = HID // K_PASS
UNITS = HID // (2 * P)
HALF = BATCH // 2

FLOPS = 2 * BATCH * (DETER * HID + (DETER + EMBED) * HID + 2 * HID * DIST)


def tile_rssmcell_pb_kernel(
    tc, h, embedding, wp1, bp1, wp2, bp2, wq1, bq1, wq2, bq2, post_mean, post_std, prior_mean, prior_std
):
    nc = tc.nc
    with ExitStack() as ctx:
        ctx.enter_context(tc.manual_schedule())
        keep = ctx.enter_context(tc.tile_pool(name="keep", bufs=1))
        ring = ctx.enter_context(tc.tile_pool(name="ring", bufs=2))
        turned = ctx.enter_context(tc.psum_pool(name="turned", bufs=5))
        sums = ctx.enter_context(tc.psum_pool(name="sums", bufs=3))

        prior = dict(name="prior", slot=0, passes=H_PASSES, w1=wp1, b1=bp1, w2=wp2, b2=bp2, mean_out=prior_mean, std_out=prior_std)
        post = dict(name="post", slot=1, passes=C_PASSES, w1=wq1, b1=bq1, w2=wq2, b2=bq2, mean_out=post_mean, std_out=post_std)

        ident = keep.tile([P, P], F32, name="ident")
        make_identity(nc, ident[:])
        zero = keep.tile([P, 1], F32, name="zero")
        one = keep.tile([P, 1], F32, name="one")
        nc.vector.memset(zero[:], 0.0)
        nc.scalar.activation(out=one[:], in_=zero[:], func=ACT.Exp)

        still = keep.tile([P, 4 * P], BF16, name="still")
        nc.vector.memset(still[:], 0.0)
        ones = keep.tile([P, P], BF16, name="ones")
        nc.vector.memset(ones[:], 1.0)
        unread = sums.tile([P, 4 * P], F32, name="total")

        def keep_clock(times):
            for repeat in range(times):
                nc.tensor.matmul(unread[:], lhsT=still[:, 0:P], rhs=still[:], start=True, stop=True)

        h_rows = keep.tile([P, ROW_TILES, DETER], BF16, name="h_rows")
        e_rows = keep.tile([P, ROW_TILES, EMBED], BF16, name="e_rows")

        def load_batch_rows(rows, source, half):
            view = source.rearrange("(p t) k -> p t k", t=ROW_TILES)
            nc.sync.dma_start(out=rows[:, 2 * half : 2 * half + 2, :], in_=view[:, 2 * half : 2 * half + 2, :])

        def load_unit(head, unit):
            features = head["passes"] * K_PASS
            rows = keep.tile([P, 2, features], BF16, name="%s_rows%d" % (head["name"], unit))
            view = head["w1"].rearrange("(g c p i) k -> g c p i k", g=HID_PASSES, c=2, p=P, i=2)
            nc.sync.dma_start(out=rows[:], in_=view[unit // 2, unit % 2])
            return rows

        load_batch_rows(h_rows, h, 0)
        prior["rows"] = [load_unit(prior, 0)]
        bias1_rows = keep.tile([P, K_PASS], BF16, name="bias1_rows")
        bias2_row = keep.tile([P, 2, DIST], BF16, name="bias2_row")
        nc.vector.memset(bias1_rows[:], 0.0)
        nc.vector.memset(bias2_row[:], 0.0)
        for head in (prior, post):
            first = HID_PASSES * head["slot"]
            nc.scalar.dma_start(
                out=bias1_rows[first : first + HID_PASSES, :], in_=head["b1"].rearrange("(g k) -> g k", g=HID_PASSES)
            )
            nc.scalar.dma_start(out=bias2_row[0:1, head["slot"], :], in_=head["b2"].unsqueeze(0))
        ident_bf = keep.tile([P, P], BF16, name="ident_bf")
        nc.vector.tensor_copy(out=ident_bf[:], in_=ident[:])

        load_batch_rows(h_rows, h, 1)
        prior["rows"].extend([load_unit(prior, unit) for unit in range(1, UNITS)])
        for half in range(2):
            load_batch_rows(e_rows, embedding, half)
        post["rows"] = [load_unit(post, unit) for unit in range(3)]
        for head in (prior, post):
            w2_rows = keep.tile([P, HID], BF16, name="%s_w2_rows" % head["name"])
            nc.sync.dma_start(out=w2_rows[:], in_=head["w2"])
            head["w2_rows"] = w2_rows
        post["rows"].append(load_unit(post, 3))

        def turn_bank(blocks):
            bank = turned.tile([P, 2, 2, P], F32, name="bank")
            for i in range(2):
                for u in range(2):
                    nc.tensor.transpose(bank[:, i, u, :], blocks[i][u], ident[:])
            return bank

        def pass_blocks(words, g):
            return [
                [words[:, i, PASS_WORDS * g + P * u : PASS_WORDS * g + P * u + P] for u in range(2)]
                for i in range(2)
            ]

        def copy_bank(engine_copy, bank, grouped_words):
            engine_copy(out=grouped_words, in_=bank[:].rearrange("p i u r -> p i r u"))

        c_codes = keep.tile([P, C_PASSES, BATCH], U32, name="c_codes", align_bytes=64)
        c_scales = keep.tile([P, C_PASSES, BATCH], U8, name="c_scales", align_bytes=64)

        def turn_batch_rows(rows, first_pass, passes, half, copies):
            words = rows[:].bitcast(F32)
            waiting = []
            for g in range(passes):
                bank = turn_bank(pass_blocks(words[:, 2 * half : 2 * half + 2, :], g))
                grouped_c = ring.tile([P, 2, P, PACK], BF16, name="grouped_w", bufs=12, align_bytes=64)
                copy_bank(copies[g], bank, grouped_c[:].bitcast(F32))
                waiting.append((first_pass + g, half, grouped_c))
            return waiting

        def quantise_batch_rows(waiting):
            for g, half, grouped_c in waiting:
                nc.vector.quantize_mx(
                    out=c_codes[:, g, HALF * half : HALF * half + HALF].bitcast(FP8X4),
                    scales=c_scales[:, g, HALF * half : HALF * half + HALF],
                    in_=grouped_c[:].rearrange("p t r j -> p (t r j)"),
                )

        def turn_weight(head, unit, pieces, copies):
            words = head["rows"][unit][:].bitcast(F32)
            waiting = []
            for g, engine_copy in zip(pieces, copies):
                bank = turn_bank(pass_blocks(words, g))
                grouped_w = ring.tile([P, 2, P, PACK], BF16, name="grouped_w", bufs=12, align_bytes=64)
                copy_bank(engine_copy, bank, grouped_w[:].bitcast(F32))
                waiting.append((head, unit, g, grouped_w))
            return waiting

        def quantise_weight(waiting):
            for head, unit, g, grouped_w in waiting:
                nc.vector.quantize_mx(
                    out=head["codes"][unit][:, g, :].bitcast(FP8X4),
                    scales=head["scales"][unit][:, g, :],
                    in_=grouped_w[:].rearrange("p i r j -> p (i r j)"),
                )

        def turn_second_weight(head):
            words = head["w2_rows"][:].bitcast(F32).rearrange("d (g u p) -> d g u p", g=HID_PASSES, u=2, p=P)
            bank = turn_bank([[words[:, g, u, :] for u in range(2)] for g in range(HID_PASSES)])
            grouped_w = ring.tile([P, 2, P, PACK], BF16, name="grouped_w", bufs=12, align_bytes=64)
            copy_bank(nc.scalar.copy, bank, grouped_w[:].bitcast(F32))
            return grouped_w

        def quantise_second_weight(head, grouped_w):
            head["w2_codes"] = keep.tile([P, HID_PASSES, DIST], U32, name="%s_w2_codes" % head["name"], align_bytes=64)
            head["w2_scales"] = keep.tile([P, HID_PASSES, DIST], U8, name="%s_w2_scales" % head["name"], align_bytes=64)
            nc.vector.quantize_mx(
                out=head["w2_codes"][:].rearrange("p g d -> p (g d)").bitcast(FP8X4),
                scales=head["w2_scales"][:].rearrange("p g d -> p (g d)"),
                in_=grouped_w[:].rearrange("p g d j -> p (g d j)"),
            )

        for head in (prior, post):
            shape = [P, head["passes"], 2 * P]
            head["codes"] = [
                keep.tile(shape, U32, name="%s_codes%d" % (head["name"], unit), align_bytes=64) for unit in range(UNITS)
            ]
            head["scales"] = [
                keep.tile(shape, U8, name="%s_scales%d" % (head["name"], unit), align_bytes=64) for unit in range(UNITS)
            ]
            head["hidden"] = [
                keep.tile([P, PACK, BATCH], BF16, name="%s_hidden%d" % (head["name"], g)) for g in range(HID_PASSES)
            ]
            head["a_codes"] = keep.tile([P, HID_PASSES, BATCH], U32, name="%s_a_codes" % head["name"], align_bytes=64)
            head["a_scales"] = keep.tile([P, HID_PASSES, BATCH], U8, name="%s_a_scales" % head["name"], align_bytes=64)

        def open_sums(head, unit, tiles, first, width):
            waiting = []
            for i in tiles:
                total = sums.tile([P, width], F32, name="total")
                waiting.append((head, unit, i, slice(first, first + width), total))
            return waiting

        def add_passes(waiting, pieces):
            for head, unit, i, columns, total in waiting:
                codes, scales = head["codes"][unit], head["scales"][unit]
                for g in pieces:
                    nc.tensor.matmul_mx(
                        out=total[:],
                        lhsT=codes[:, g, P * i : P * i + P].bitcast(FP8X4),
                        lhsT_scale=scales[:, g, P * i : P * i + P],
                        rhs=c_codes[:, g, columns].bitcast(FP8X4),
                        rhs_scale=c_scales[:, g, columns],
                        start=(g == 0),
                        stop=(g == head["passes"] - 1),
                    )

        def first_layer(head, unit, tiles, first, width):
            waiting = []
            for i in tiles:
                one = open_sums(head, unit, (i,), first, width)
                add_passes(one, range(head["passes"]))
                waiting.extend(one)
            return waiting

        def empty_sums(waiting, on_scalar):
            for head, unit, i, columns, total in waiting:
                j = 2 * (unit % 2) + i
                bias = bias1[:, HID_PASSES * head["slot"] + unit // 2, j : j + 1]
                rounded = head["hidden"][unit // 2][:, j, columns]
                if on_scalar:
                    nc.scalar.activation(out=rounded, in_=total[:], func=ACT.Relu, bias=bias, scale=1.0)
                else:
                    nc.vector.tensor_scalar(
                        out=rounded, in0=total[:], scalar1=bias, scalar2=0.0, op0=ALU.add, op1=ALU.max
                    )

        def group_hidden(head, g, first, width):
            grouped_a = ring.tile([P, width, PACK], BF16, name="grouped_a", bufs=3, align_bytes=64)
            nc.vector.tensor_copy(
                out=grouped_a[:].rearrange("p (c i) j -> p c j i", i=4),
                in_=head["hidden"][g][:, :, first : first + width].rearrange("p j (c i) -> p c j i", i=4),
            )
            return grouped_a

        def quantise_hidden(head, g, first, width, grouped_a):
            nc.vector.quantize_mx(
                out=head["a_codes"][:, g, first : first + width].bitcast(FP8X4),
                scales=head["a_scales"][:, g, first : first + width],
                in_=grouped_a[:].rearrange("p b j -> p (b j)"),
            )

        def second_layer(head, first_tile, tiles):
            result = turned.tile([P, tiles, DIST], F32, name="bank")
            for n in range(tiles):
                t = first_tile + n
                for g in range(HID_PASSES):
                    nc.tensor.matmul_mx(
                        out=result[:, n, :],
                        lhsT=head["a_codes"][:, g, P * t : P * t + P].bitcast(FP8X4),
                        lhsT_scale=head["a_scales"][:, g, P * t : P * t + P],
                        rhs=head["w2_codes"][:, g, :].bitcast(FP8X4),
                        rhs_scale=head["w2_scales"][:, g, :],
                        start=(g == 0),
                        stop=(g == HID_PASSES - 1),
                    )
            return result

        def spread_bias2(head, columns, tiles):
            return bias2[:, head["slot"], columns].unsqueeze(1).to_broadcast([P, tiles, STOC])

        def by_partition(out):
            return out.rearrange("(p t) d -> p t d", t=ROW_TILES)

        for head in (prior, post):
            for part in ("v", "size", "decay", "mean", "hinge"):
                head[part] = keep.tile([P, ROW_TILES, STOC], F32, name="%s_%s" % (head["name"], part))

        bias1 = keep.tile([P, 2 * HID_PASSES, PACK], F32, name="bias1")
        bias2 = keep.tile([P, 2, DIST], F32, name="bias2")

        def spread_biases():
            columns = bias1_rows[:].rearrange("r (c p i) -> r c i p", c=2, i=2)
            turned_rows = turned.tile([P, PACK, P], BF16, name="bank")
            for j in range(PACK):
                nc.tensor.transpose(turned_rows[:, j, :], columns[:, j // 2, j % 2, :], ident_bf[:])
            nc.vector.tensor_copy(
                out=bias1[:], in_=turned_rows[:, :, 0 : 2 * HID_PASSES].rearrange("p j r -> p r j")
            )
            spread = turned.tile([P, 2, DIST], F32, name="bank")
            nc.tensor.matmul(
                spread[:].rearrange("p s d -> p (s d)"),
                lhsT=ones[:],
                rhs=bias2_row[:].rearrange("p s d -> p (s d)"),
                start=True,
                stop=True,
            )
            nc.vector.tensor_copy(out=bias2[:], in_=spread[:])

        def add_bias(head, first_tile, tiles, result):
            nc.vector.tensor_tensor(
                out=head["v"][:, first_tile : first_tile + tiles, :],
                in0=result[:, :, STOC:DIST],
                in1=spread_bias2(head, slice(STOC, DIST), tiles),
                op=ALU.add,
            )

        def last_decay_of(head, first_tile, tiles):
            span = slice(first_tile, first_tile + tiles)
            v, size, decay = [head[part][:, span, :] for part in ("v", "size", "decay")]
            nc.vector.scalar_tensor_tensor(out=size, in0=v, scalar=-1.0, in1=v, op0=ALU.mult, op1=ALU.min)
            nc.scalar.activation(out=decay, in_=size, func=ACT.Exp)

        def decay_of(head, first_tile, tiles):
            span = slice(first_tile, first_tile + tiles)
            v, size, decay = [head[part][:, span, :] for part in ("v", "size", "decay")]
            nc.scalar.activation(out=size, in_=v, func=ACT.Abs)
            nc.scalar.activation(out=decay, in_=size, func=ACT.Exp, scale=-1.0)

        def mean_and_hinge(head, first_tile, tiles, result):
            span = slice(first_tile, first_tile + tiles)
            v, mean, hinge = [head[part][:, span, :] for part in ("v", "mean", "hinge")]
            nc.vector.tensor_tensor(
                out=mean, in0=result[:, :, 0:STOC], in1=spread_bias2(head, slice(0, STOC), tiles), op=ALU.add
            )
            nc.sync.dma_start(out=by_partition(head["mean_out"])[:, span, :], in_=mean)
            nc.vector.tensor_scalar(out=hinge, in0=v, scalar1=0.0, scalar2=0.1, op0=ALU.max, op1=ALU.add)

        def finish_outputs(head):
            name = head["name"]
            log_term = keep.tile([P, ROW_TILES, STOC], F32, name="%s_log" % name)
            nc.scalar.activation(out=log_term[:], in_=head["decay"][:], func=ACT.Ln, bias=1.0)
            std = keep.tile([P, ROW_TILES, STOC], F32, name="%s_std" % name)
            nc.vector.tensor_tensor(out=std[:], in0=head["hinge"][:], in1=log_term[:], op=ALU.add)
            nc.sync.dma_start(out=by_partition(head["std_out"]), in_=std[:])

        both = (0, 1)
        S, V = nc.scalar.copy, nc.vector.tensor_copy
        keep_clock(6)
        h0 = turn_batch_rows(h_rows, 0, H_PASSES, 0, (S, V))
        keep_clock(1)
        quantise_batch_rows(h0)
        p0 = turn_weight(prior, 0, range(2), (S, V))
        spread_biases()
        keep_clock(1)
        quantise_weight(p0)
        h1 = turn_batch_rows(h_rows, 0, H_PASSES, 1, (S, V))
        keep_clock(1)
        m0 = first_layer(prior, 0, both, 0, HALF)
        quantise_batch_rows(h1)
        empty_sums(m0[:1], True)
        empty_sums(m0[1:], False)
        p1 = turn_weight(prior, 1, range(2), (S, V))
        m0 = first_layer(prior, 0, both, HALF, HALF)
        quantise_weight(p1)
        empty_sums(m0[:1], True)
        empty_sums(m0[1:], False)
        p2 = turn_weight(prior, 2, range(2), 3 * (S,))
        m1 = first_layer(prior, 1, both, 0, BATCH)
        quantise_weight(p2)
        empty_sums(m1[:1], True)
        empty_sums(m1[1:], False)
        p3 = turn_weight(prior, 3, range(2), 3 * (S,))
        quantise_weight(p3)
        m2 = first_layer(prior, 2, (0,), 0, BATCH)
        empty_sums(m2, True)
        e0 = turn_batch_rows(e_rows, H_PASSES, C_PASSES - H_PASSES, 0, (S, V, S))
        quantise_batch_rows(e0)
        m3 = first_layer(prior, 2, (1,), 0, BATCH)
        empty_sums(m3, True)
        e1 = turn_batch_rows(e_rows, H_PASSES, C_PASSES - H_PASSES, 1, (V, S, S))
        quantise_batch_rows(e1)
        m2 = first_layer(prior, 3, (0,), 0, BATCH)
        empty_sums(m2, False)
        q0a = turn_weight(post, 0, range(3), 3 * (S,))
        quantise_weight(q0a)
        m3 = first_layer(prior, 3, (1,), 0, BATCH)
        empty_sums(m3, False)
        q0b = turn_weight(post, 0, (3, 4), 3 * (S,))
        n0 = open_sums(post, 0, both, 0, BATCH)
        add_passes(n0, range(H_PASSES))
        quantise_weight(q0b)
        q1a = turn_weight(post, 1, range(3), 3 * (S,))
        quantise_weight(q1a)
        add_passes(n0[:1], range(H_PASSES, C_PASSES))
        empty_sums(n0[:1], True)
        q1b = turn_weight(post, 1, (3, 4), 3 * (S,))
        grouped_p0 = group_hidden(prior, 0, 0, BATCH)
        quantise_weight(q1b)
        add_passes(n0[1:], range(H_PASSES, C_PASSES))
        m3 = n0[1:]
        empty_sums(m3, True)
        q2a = turn_weight(post, 2, range(3), 3 * (S,))
        quantise_hidden(prior, 0, 0, BATCH, grouped_p0)
        quantise_weight(q2a)
        m2 = first_layer(post, 1, (0,), 0, BATCH)
        empty_sums(m2, True)
        q2b = turn_weight(post, 2, (3, 4), 3 * (S,))
        grouped_p1 = group_hidden(prior, 1, 0, BATCH)
        quantise_weight(q2b)
        m3 = first_layer(post, 1, (1,), 0, BATCH)
        empty_sums(m3, True)
        w2p = turn_second_weight(prior)
        w2q = turn_second_weight(post)
        q3a = turn_weight(post, 3, range(2), 3 * (S,))
        quantise_hidden(prior, 1, 0, BATCH, grouped_p1)
        quantise_second_weight(prior, w2p)
        quantise_second_weight(post, w2q)
        m2 = first_layer(post, 2, (0,), 0, BATCH)
        empty_sums(m2, True)
        quantise_weight(q3a)
        grouped_q0 = group_hidden(post, 0, 0, BATCH)
        q3b = turn_weight(post, 3, (2, 3, 4), 3 * (S,))
        prior_result = second_layer(prior, 0, ROW_TILES)
        m3 = first_layer(post, 2, (1,), 0, BATCH)
        quantise_weight(q3b)
        quantise_hidden(post, 0, 0, BATCH, grouped_q0)
        add_bias(prior, 0, ROW_TILES, prior_result)
        mean_and_hinge(prior, 0, ROW_TILES, prior_result)
        empty_sums(m3, True)
        m4 = first_layer(post, 3, both, 0, HALF)
        empty_sums(m4[:1], True)
        empty_sums(m4[1:], False)
        decay_of(prior, 0, ROW_TILES)
        m5 = first_layer(post, 3, both, 2 * P, P)
        grouped_a = group_hidden(post, 1, 0, HALF)
        empty_sums(m5, True)
        m6 = first_layer(post, 3, both, 3 * P, P)
        empty_sums(m6, True)
        grouped_b = group_hidden(post, 1, 2 * P, P)
        quantise_hidden(post, 1, 0, HALF, grouped_a)
        grouped_c = group_hidden(post, 1, 3 * P, P)
        quantise_hidden(post, 1, 2 * P, P, grouped_b)
        first_result = second_layer(post, 0, 2)
        quantise_hidden(post, 1, 3 * P, P, grouped_c)
        second_result = second_layer(post, 2, 1)
        third_result = second_layer(post, 3, 1)
        add_bias(post, 0, 2, first_result)
        decay_of(post, 0, 2)
        add_bias(post, 2, 1, second_result)
        decay_of(post, 2, 1)
        add_bias(post, 3, 1, third_result)
        last_decay_of(post, 3, 1)
        mean_and_hinge(post, 0, 2, first_result)
        mean_and_hinge(post, 2, 1, second_result)
        mean_and_hinge(post, 3, 1, third_result)
        finish_outputs(post)
        finish_outputs(prior)
